import numpy as np
import ml_dtypes


def mxq(x, axis, fmt="e4m3"):
    dtype, down = {"e4m3": (ml_dtypes.float8_e4m3fn, 7), "e5m2": (ml_dtypes.float8_e5m2, 14)}[fmt]
    v = np.moveaxis(np.asarray(x, np.float32).astype(ml_dtypes.bfloat16).astype(np.float64), axis, -1)
    blocks = v.reshape(v.shape[:-1] + (-1, 32))
    amax = np.abs(blocks).max(-1, keepdims=True)
    byte = np.maximum(np.where(amax > 0, np.frexp(amax)[1] - 1 + 127, 0) - down, 1)
    scale = np.exp2(byte - 127.0)
    codes = (blocks / scale).astype(np.float32).astype(dtype).astype(np.float64)
    return np.moveaxis((codes * scale).reshape(v.shape), -1, axis)


WIDE = False


def mx_kscale(k):
    if not WIDE:
        return np.ones(k)
    levels = np.array([10, -10, 5, -5, 0])
    if k % 512:
        return np.exp2(np.random.permutation(np.resize(levels, k // 32))).repeat(32)
    a = np.empty((k // 512, 16))
    for p in range(k // 512):
        a[p, :8] = np.random.permutation(np.resize(levels, 8))
        for g in range(8):
            far = levels[np.abs(levels - a[p, g]) >= 10]
            a[p, g + 8] = far[np.random.randint(len(far))]
    return np.exp2(a.ravel()).repeat(32)


BF16 = ml_dtypes.bfloat16


def bf(x):
    return np.asarray(x, np.float32).astype(BF16)


def f64(x):
    return np.asarray(x).astype(np.float64)


B, CL, CH, CK, CV, CO, H, W = 2, 1024, 2048, 256, 512, 1024, 24, 24
N = H * W
CF = CO + CH
EPS = 1e-5


def draw0():
    s = mx_kscale(CV)
    t = mx_kscale(CF)
    tc, th = t[:CO], t[CO:]
    return {"context": bf(np.random.standard_normal((B, CV, H, W)) * 0.4 * s[None, :, None, None]),
            "high_feats": bf(np.random.standard_normal((B, CH, H, W)) * th[None, :, None, None]),
            "ww": bf(np.random.standard_normal((CO, CV)) * 2.0 / np.sqrt(CV) / s[None, :] * tc[:, None]),
            "bw": bf(np.random.standard_normal(CO) * 0.3 * tc),
            "wf": bf(np.random.standard_normal((CO, CF)) / np.sqrt(CF) / t[None, :]),
            "bfuse": bf(np.random.standard_normal(CO) * 0.3),
            "gf": bf(np.random.uniform(0.5, 1.5, CO)),
            "bef": bf(np.random.standard_normal(CO) * 0.3),
            "mf": bf(np.random.standard_normal(CO) * 0.3),
            "vf": bf(np.random.uniform(0.5, 1.5, CO))}


def core(context, high_feats, ww, bw, wf, bfuse, gf, bef, mf, vf):
    ctx = f64(context).reshape(B, CV, N)
    hi = f64(high_feats).reshape(B, CH, N)
    c = (mxq(f64(ww), 1, "e4m3") @ mxq(ctx, 1, "e4m3")) + f64(bw)[None, :, None]
    fused = np.concatenate([c, hi], axis=1)
    y = (mxq(f64(wf), 1, "e4m3") @ mxq(fused, 1, "e4m3")) + f64(bfuse)[None, :, None]
    sc = f64(gf) / np.sqrt(f64(vf) + EPS)
    out = (y - f64(mf)[None, :, None]) * sc[None, :, None] + f64(bef)[None, :, None]
    return out.reshape(B, CO, H, W)


def e4m3fn_bytes(y):
    return np.clip(np.asarray(y, np.float64), -448.0, 448.0).astype(np.float32).astype(ml_dtypes.float8_e4m3fn).view(np.uint8)


def e4m3fn_values(b):
    return np.asarray(b, np.uint8).view(ml_dtypes.float8_e4m3fn).astype(np.float64)


def setup_inputs():
    d = draw0()
    x0 = np.asarray(d['wf']).astype(np.float64)
    s = (np.max(np.abs(x0), axis=(0,), keepdims=True) / 448.0).astype(np.float32)
    out = {}
    for k, v in d.items():
        if k == 'wf':
            out['wf_bytes'] = e4m3fn_bytes(x0 / s.astype(np.float64))
            out['wf_scale'] = s
        else:
            out[k] = v
    return out


def reference(context, high_feats, ww, bw, wf_bytes, wf_scale, bfuse, gf, bef, mf, vf):
    return core(context, high_feats, ww, bw, e4m3fn_values(wf_bytes) * wf_scale.astype(np.float64), bfuse, gf, bef, mf, vf)

@@ -1,0 +1,631 @@
+from contextlib import ExitStack
+
+import concourse.mybir as mybir
+from concourse.masks import make_identity
+
+F32 = mybir.dt.float32
+BF16 = mybir.dt.bfloat16
+U32 = mybir.dt.uint32
+U8 = mybir.dt.uint8
+FP8 = mybir.dt.float8_e4m3fn
+FP8X4 = mybir.dt.float8_e4m3fn_x4
+MULT = mybir.AluOpType.mult
+ADD = mybir.AluOpType.add
+SUB = mybir.AluOpType.subtract
+POW = mybir.AluOpType.pow
+IDENT = mybir.ActivationFunctionType.Identity
+
+P = 128
+B, CV, CH, CO, HW = 2, 512, 2048, 1024, 576
+CF = CO + CH
+N = B * HW
+MT = CO // P
+NQ = MT // 2
+GC = CO // 512
+GH = CH // 512
+G = GC + GH
+EPS = 1e-5
+FLOPS = 2 * CO * CV * N + 2 * CO * CF * N
+
+X, Z, Y = (0, 512), (512, 128), (640, 512)
+CTX = -1
+
+
+def tile_afnb_pb_kernel(tc, context, high, ww, bw, wf_bytes, wf_scale, bfuse, gf, bef, mf, vf, out):
+    nc = tc.nc
+    with ExitStack() as ctx:
+        keep = ctx.enter_context(tc.tile_pool(name="keep", bufs=1))
+        rot = ctx.enter_context(tc.tile_pool(name="rot", bufs=3))
+        psum = ctx.enter_context(tc.psum_pool(name="psum", bufs=4))
+
+        wf_t = wf_bytes.rearrange("(q m p) k -> q p m k", p=P, m=2)
+        ww_t = ww.rearrange("(g p t) k -> g p t k", g=GC, t=4)
+        ctx_t = context.rearrange("b (p t) h w -> b p t (h w)", t=4)
+        high_t = high.rearrange("b (g p t) h w -> b g p t (h w)", p=P, t=4)
+        wbytes, raws = {}, {}
+        wwr = keep.tile([P, GC, 4, CV], BF16, name="wwr")
+
+        def load_w(q, m, lo=0, hi=CF):
+            if q not in wbytes:
+                wbytes[q] = rot.tile([P, 2, CF], U8, name="wbytes", bufs=3)
+            nc.sync.dma_start(out=wbytes[q][:, m, lo:hi], in_=wf_t[q, :, m, lo:hi])
+
+        def load_ww(g):
+            nc.sync.dma_start(out=wwr[:, g], in_=ww_t[g])
+
+        def load_act(g, b):
+            raws[g, b] = rot.tile([P, 4, HW], BF16, name="raw", bufs=7)
+            nc.sync.dma_start(out=raws[g, b][:], in_=ctx_t[b] if g == CTX else high_t[b, g])
+
+        ident = keep.tile([P, P], F32, name="ident")
+        rows = keep.tile([P, P], BF16, name="rows")
+        rows32 = keep.tile([P, P], F32, name="rows32")
+        ws = keep.tile([P, G, 4], F32, name="ws")
+        bwt = keep.tile([P, GC, 4], BF16, name="bwt")
+        bn = keep.tile([P, 5 * MT], F32, name="bn")
+        bn_scale = keep.tile([P, MT], F32, name="bn_scale")
+        bn_bias = keep.tile([P, MT], F32, name="bn_bias")
+        half = keep.tile([P, MT], F32, name="half")
+        rstd = keep.tile([P, MT], F32, name="rstd")
+        bdiff = keep.tile([P, MT], F32, name="bdiff")
+
+        def load_consts():
+            nc.gpsimd.memset(rows[:], 0.0)
+            for i, v in enumerate((bfuse, gf, bef, mf, vf)):
+                nc.gpsimd.dma_start(out=rows[MT * i : MT * (i + 1), :], in_=v.rearrange("(m p) -> m p", p=P))
+            nc.scalar.dma_start(out=ws[:], in_=wf_scale.rearrange("o (g p t) -> p (o g) t", p=P, t=4))
+            nc.scalar.dma_start(out=bwt[:], in_=bw.rearrange("(g p t) -> p g t", p=P, t=4))
+            make_identity(nc, ident[:])
+            nc.gpsimd.tensor_copy(out=rows32[:], in_=rows[:])
+            nc.gpsimd.memset(half[:], -0.5)
+
+        const_bank = []
+
+        def tr_consts():
+            bank = psum.tile([P, 2, 2 * P], F32, name="tr")
+            const_bank.append(bank)
+            nc.tensor.transpose(bank[:, 0, 0:P], rows32[:], ident[:])
+
+        def exit_consts():
+            nc.scalar.copy(out=bn[:], in_=const_bank[0][:, 0, 0 : 5 * MT])
+
+        def consts():
+            col = [bn[:, MT * i : MT * (i + 1)] for i in range(5)]
+            nc.gpsimd.tensor_scalar(out=rstd[:], in0=col[4], scalar1=EPS, scalar2=None, op0=ADD)
+            nc.gpsimd.tensor_tensor(out=rstd[:], in0=rstd[:], in1=half[:], op=POW)
+            nc.gpsimd.tensor_tensor(out=bn_scale[:], in0=col[1], in1=rstd[:], op=MULT)
+            nc.gpsimd.tensor_tensor(out=bdiff[:], in0=col[0], in1=col[3], op=SUB)
+            nc.gpsimd.tensor_tensor(out=bdiff[:], in0=bdiff[:], in1=bn_scale[:], op=MULT)
+            nc.gpsimd.tensor_tensor(out=bn_bias[:], in0=bdiff[:], in1=col[2], op=ADD)
+
+        def quant(codes, scales, src, lo, n):
+            nc.vector.quantize_mx(out=codes[:, lo : lo + n].bitcast(FP8X4), scales=scales[:, lo : lo + n], in_=src)
+
+        act_c = [keep.tile([P, N], U32, name="act_c%d" % g, align_bytes=64) for g in range(G)]
+        act_s = [keep.tile([P, N], U8, name="act_s%d" % g, align_bytes=64) for g in range(G)]
+        ctx_c = keep.tile([P, N], U32, name="ctx_c", align_bytes=64)
+        ctx_s = keep.tile([P, N], U8, name="ctx_s", align_bytes=64)
+        grps = {}
+
+        def inter(g, b, eng="s", lo=0, hi=HW):
+            if (g, b) not in grps:
+                grps[g, b] = rot.tile([P, HW, 4], BF16, name="grp", bufs=3, align_bytes=64)
+            dst = grps[g, b][:, lo:hi, :]
+            src = raws[g, b][:, :, lo:hi].rearrange("p t n -> p n t")
+            if eng == "v":
+                nc.vector.tensor_copy(out=dst, in_=src)
+            else:
+                nc.scalar.copy(out=dst, in_=src)
+
+        def quant_act(g, b):
+            c, s = (ctx_c, ctx_s) if g == CTX else (act_c[GC + g], act_s[GC + g])
+            flat = grps[g, b][:].rearrange("p n t -> p (n t)")
+            quant(c, s, flat[:, 0:2048], b * HW, 512)
+            quant(c, s, flat[:, 2048:2304], b * HW + 512, 64)
+
+        wwg = keep.tile([P, GC * 4, 512], BF16, name="wwg", align_bytes=64)
+        wwc = keep.tile([P, CO], U32, name="wwc", align_bytes=64)
+        wwsc = keep.tile([P, CO], U8, name="wwsc", align_bytes=64)
+        ww_bank = {}
+
+        def tr_ww(i):
+            ww_bank[i] = psum.tile([P, 2, 2, P], F32, name="tr")
+            for j in range(2):
+                g, t = divmod(2 * i + j, 4)
+                words = wwr[:, g, t, :].bitcast(F32)
+                for u in range(2):
+                    nc.tensor.transpose(ww_bank[i][:, j, u, :], words[:, u : CV // 2 : 2], ident[:])
+
+        def exit_ww(i):
+            nc.scalar.copy(
+                out=wwg[:, 2 * i : 2 * i + 2, :].bitcast(F32).rearrange("p c (r u) -> p c r u", u=2),
+                in_=ww_bank[i][:].rearrange("p c u r -> p c r u"),
+            )
+
+        def quant_ww(g):
+            quant(wwc, wwsc, wwg[:, 4 * g : 4 * g + 4, :].rearrange("p c k -> p (c k)"), 512 * g, 512)
+
+        cgrp, cbank = {}, {}
+
+        def stage1(g, nb):
+            bank = psum.tile([P, 4, P], F32, name="acc")
+            cbank[g, nb] = bank
+            n = slice(nb * P, (nb + 1) * P)
+            for t in range(4):
+                k = slice((4 * g + t) * P, (4 * g + t + 1) * P)
+                nc.tensor.matmul_mx(
+                    out=bank[:, t, :], lhsT=wwc[:, k].bitcast(FP8X4), lhsT_scale=wwsc[:, k],
+                    rhs=ctx_c[:, n].bitcast(FP8X4), rhs_scale=ctx_s[:, n], start=True, stop=True)
+
+        def exit_c(g, nb):
+            lo, n = X if nb < 4 else Z if nb < 5 else Y
+            if (g, lo) not in cgrp:
+                cgrp[g, lo] = rot.tile([P, n, 4], BF16, name="cgrp", bufs=3, align_bytes=64)
+            off = nb * P - lo
+            nc.vector.tensor_tensor(
+                out=cgrp[g, lo][:, off : off + P, :], in0=cbank[g, nb][:].rearrange("p t n -> p n t"),
+                in1=bwt[:, g, :].unsqueeze(1).to_broadcast([P, P, 4]), op=ADD)
+
+        def quant_c(g, chunk):
+            lo, n = chunk
+            quant(act_c[g], act_s[g], cgrp[g, lo][:].rearrange("p n t -> p (n t)"), lo, n)
+
+        wb, wg, wbank = {}, {}, {}
+        wc = [keep.tile([P, G, 2 * P], U32, name="wc%d" % q, align_bytes=64) for q in range(NQ)]
+        wsc = [keep.tile([P, G, 2 * P], U8, name="wsc%d" % q, align_bytes=64) for q in range(NQ)]
+
+        def cast_w(q, h):
+            wb[q, h] = rot.tile([P, 2, 1024], BF16, name="wb", bufs=4)
+            for m in range(2):
+                nc.scalar.copy(out=wb[q, h][:, m], in_=wbytes[q][:, m, 1024 * h : 1024 * (h + 1)].bitcast(FP8))
+
+        def tr_w(q, g):
+            h, j = divmod(g, 2)
+            bank = psum.tile([P, 2, 2 * P], F32, name="tr")
+            wbank[q, g] = bank
+            for m in range(2):
+                words = wb[q, h][:, m].bitcast(F32)
+                for u in range(2):
+                    nc.tensor.transpose(bank[:, u, m * P : (m + 1) * P], words[:, 256 * j + u : 256 * (j + 1) : 2], ident[:])
+
+        def prod_w(q, g):
+            h, j = divmod(g, 2)
+            if (q, h) not in wg:
+                wg[q, h] = rot.tile([P, 2, 1024], BF16, name="wg", bufs=3, align_bytes=64)
+            nc.vector.tensor_tensor(
+                out=wg[q, h][:, j].rearrange("p (r u e) -> p r u e", u=2, e=2),
+                in0=wbank[q, g][:].bitcast(BF16).rearrange("p u (r e) -> p r u e", e=2),
+                in1=ws[:, g, :].rearrange("p (u e) -> p u e", e=2).unsqueeze(1).to_broadcast([P, 2 * P, 2, 2]),
+                op=MULT)
+
+        planes = {}
+
+        def prod_s(q, g):
+            planes[q, g] = rot.tile([P, 4, 2 * P], BF16, name="plane", bufs=3)
+            pairs = wbank[q, g][:].bitcast(BF16)
+            for t in range(4):
+                nc.scalar.activation(out=planes[q, g][:, t, :], in_=pairs[:, t // 2, t % 2 : 4 * P : 2],
+                                     func=mybir.ActivationFunctionType.Copy, scale=ws[:, g, t : t + 1])
+
+        def inter_w(q, g):
+            h, j = divmod(g, 2)
+            if (q, h) not in wg:
+                wg[q, h] = rot.tile([P, 2, 1024], BF16, name="wg", bufs=3, align_bytes=64)
+            nc.vector.tensor_copy(out=wg[q, h][:, j].rearrange("p (r t) -> p r t", t=4),
+                                  in_=planes[q, g][:].rearrange("p t r -> p r t"))
+
+        def quant_w(q, h):
+            flat = wg[q, h][:].rearrange("p j k -> p (j k)")
+            quant(wc[q][:].rearrange("p g r -> p (g r)"), wsc[q][:].rearrange("p g r -> p (g r)"), flat, 512 * h, 512)
+
+        out_v = out.rearrange("b (m p) h w -> m b p (h w)", p=P)
+        accs, outs = {}, {}
+
+        def mx(m, chunk, g, tag="acc"):
+            lo, n = chunk
+            if (m, lo) not in accs:
+                accs[m, lo] = [psum.tile([P, n], F32, name=tag), 0]
+            acc, done = accs[m, lo]
+            q, r = divmod(m, 2)
+            k = slice(r * P, (r + 1) * P)
+            nc.tensor.matmul_mx(
+                out=acc[:], lhsT=wc[q][:, g, k].bitcast(FP8X4), lhsT_scale=wsc[q][:, g, k],
+                rhs=act_c[g][:, lo : lo + n].bitcast(FP8X4), rhs_scale=act_s[g][:, lo : lo + n],
+                start=(done == 0), stop=(done == G - 1))
+            accs[m, lo][1] = done + 1
+
+        def leave(m, chunk, eng="s"):
+            lo, n = chunk
+            part = 0 if lo == 0 else 1
+            if (m, part) not in outs:
+                outs[m, part] = rot.tile([P, (512, 640)[part]], F32, name="out%d" % part, bufs=4)
+            dst = outs[m, part][:, lo - 512 * part : lo - 512 * part + n]
+            acc = accs[m, lo][0]
+            if eng == "v":
+                nc.vector.tensor_scalar(out=dst, in0=acc[:], scalar1=bn_scale[:, m : m + 1], scalar2=bn_bias[:, m : m + 1], op0=MULT, op1=ADD)
+            else:
+                nc.scalar.activation(out=dst, in_=acc[:], func=IDENT, bias=bn_bias[:, m : m + 1], scale=bn_scale[:, m : m + 1])
+
+        def store(m, part):
+            if part == 0:
+                nc.sync.dma_start(out=out_v[m, 0, :, 0:512], in_=outs[m, 0][:])
+            elif part == 1:
+                nc.sync.dma_start(out=out_v[m, 0, :, 512:576], in_=outs[m, 1][:, 0:64])
+            else:
+                nc.sync.dma_start(out=out_v[m, 1], in_=outs[m, 1][:, 64:640])
+
+        load_consts()
+        load_w(0, 1, 0, 1024)
+        load_w(0, 0, 0, 1024)
+        load_act(CTX, 0)
+        load_w(0, 0, 1024, 2048)
+        load_w(0, 1, 1024, 2048)
+        load_ww(1)
+        load_w(0, 1, 2048, 3072)
+        load_act(CTX, 1)
+        load_act(0, 0)
+        load_ww(0)
+        load_w(0, 0, 2048, 3072)
+        load_w(1, 1)
+        load_w(1, 0)
+        load_w(2, 0)
+        load_act(1, 0)
+        load_act(3, 1)
+        load_act(3, 0)
+        load_w(3, 1)
+        load_act(2, 0)
+        load_act(0, 1)
+        load_w(2, 1)
+        load_act(2, 1)
+        load_act(1, 1)
+        load_w(3, 0)
+        with tc.manual_schedule(engines={mybir.EngineType.PE, mybir.EngineType.DVE, mybir.EngineType.Activation}):
+            cast_w(0, 0)
+            inter(CTX, 0, "v", 0, 288)
+            inter(CTX, 0, "s", 288, 576)
+            tr_w(0, 0)
+            tr_w(0, 1)
+            prod_w(0, 0)
+            cast_w(0, 1)
+            tr_ww(3)
+            prod_w(0, 1)
+            tr_ww(2)
+            exit_ww(3)
+            tr_w(0, 3)
+            quant_act(CTX, 0)
+            exit_ww(2)
+            tr_w(0, 2)
+            inter(CTX, 1, "s", 0, 288)
+            quant_ww(1)
+            prod_w(0, 3)
+            stage1(1, 0)
+            stage1(1, 3)
+            inter(CTX, 1, "s", 288, 576)
+            stage1(1, 2)
+            prod_w(0, 2)
+            tr_ww(1)
+            tr_ww(0)
+            exit_ww(1)
+            exit_c(1, 0)
+            tr_consts()
+            stage1(1, 1)
+            exit_ww(0)
+            quant_w(0, 1)
+            cast_w(1, 2)
+            quant_ww(0)
+            exit_c(1, 3)
+            stage1(0, 0)
+            cast_w(0, 2)
+            quant_act(CTX, 1)
+            stage1(0, 2)
+            exit_c(1, 2)
+            cast_w(1, 1)
+            tr_w(0, 5)
+            exit_c(1, 1)
+            stage1(0, 3)
+            exit_c(0, 0)
+            exit_consts()
+            stage1(1, 8)
+            cast_w(1, 0)
+            consts()
+            tr_w(0, 4)
+            quant_w(0, 0)
+            stage1(0, 6)
+            exit_c(0, 2)
+            inter(0, 0, "s", 288, 576)
+            exit_c(1, 8)
+            stage1(0, 1)
+            tr_w(1, 3)
+            exit_c(0, 3)
+            inter(0, 0, "s", 0, 288)
+            tr_w(1, 5)
+            exit_c(0, 1)
+            stage1(0, 8)
+            quant_c(1, X)
+            stage1(1, 4)
+            inter(1, 0, "s", 0, 288)
+            quant_c(0, X)
+            exit_c(0, 8)
+            quant_act(0, 0)
+            inter(1, 0, "s", 288, 576)
+            exit_c(0, 6)
+            prod_w(0, 5)
+            mx(0, X, 2)
+            inter(2, 0, "s", 0, 288)
+            mx(1, X, 2)
+            prod_w(1, 3)
+            tr_w(1, 2)
+            inter(3, 0, "s", 0, 288)
+            mx(0, X, 0)
+            stage1(1, 5)
+            prod_w(0, 4)
+            mx(1, X, 0)
+            inter(3, 0, "s", 288, 576)
+            quant_act(1, 0)
+            tr_w(1, 4)
+            exit_c(1, 4)
+            mx(0, X, 1)
+            inter(2, 0, "s", 288, 576)
+            mx(0, X, 3)
+            prod_w(1, 5)
+            tr_w(1, 1)
+            mx(1, X, 1)
+            quant_act(3, 0)
+            cast_w(2, 2)
+            mx(1, X, 3)
+            quant_w(0, 2)
+            tr_w(1, 0)
+            quant_act(2, 0)
+            inter(1, 1, "s", 288, 576)
+            stage1(1, 6)
+            exit_c(1, 6)
+            mx(1, X, 4)
+            mx(0, X, 4)
+            prod_w(1, 2)
+            cast_w(2, 1)
+            mx(1, X, 5)
+            mx(0, X, 5)
+            prod_w(1, 4)
+            tr_w(2, 4)
+            inter(0, 1, "s", 288, 576)
+            exit_c(1, 5)
+            tr_w(2, 2)
+            leave(0, X, "s")
+            quant_w(1, 1)
+            leave(1, X, "s")
+            stage1(0, 5)
+            prod_w(1, 0)
+            inter(1, 1, "s", 0, 288)
+            stage1(1, 7)
+            mx(3, X, 2)
+            mx(2, X, 2)
+            quant_w(1, 2)
+            mx(2, X, 3)
+            prod_w(1, 1)
+            inter(0, 1, "s", 0, 288)
+            mx(3, X, 3)
+            mx(3, X, 4)
+            exit_c(0, 5)
+            tr_w(2, 3)
+            inter(2, 1, "s", 288, 576)
+            exit_c(1, 7)
+            mx(2, X, 4)
+            mx(3, X, 5)
+            quant_w(1, 0)
+            stage1(0, 7)
+            mx(2, X, 5)
+            quant_act(0, 1)
+            inter(2, 1, "s", 0, 288)
+            mx(3, X, 0)
+            mx(2, X, 0)
+            exit_c(0, 7)
+            mx(3, X, 1)
+            mx(2, X, 1)
+            quant_act(1, 1)
+            tr_w(2, 5)
+            leave(3, X, "s")
+            quant_c(1, Y)
+            leave(2, X, "s")
+            stage1(0, 4)
+            store(3, 0)
+            store(0, 0)
+            mx(0, Y, 2)
+            inter(3, 1, "s", 0, 288)
+            quant_c(0, Y)
+            mx(2, Y, 2)
+            store(2, 0)
+            store(1, 0)
+            mx(1, Y, 2)
+            exit_c(0, 4)
+            mx(0, Y, 3)
+            mx(2, Y, 3)
+            quant_act(2, 1)
+            mx(1, Y, 3)
+            inter(3, 1, "s", 288, 576)
+            mx(0, Y, 0)
+            mx(2, Y, 0)
+            prod_w(2, 2)
+            mx(0, Y, 1)
+            mx(2, Y, 1)
+            mx(1, Y, 0)
+            cast_w(2, 0)
+            mx(0, Y, 4)
+            quant_act(3, 1)
+            mx(1, Y, 1)
+            mx(3, Z, 2)
+            mx(2, Y, 4)
+            quant_c(0, Z)
+            mx(3, Z, 3)
+            mx(1, Y, 4)
+            prod_w(2, 4)
+            cast_w(3, 0)
+            mx(3, Z, 4)
+            mx(0, Y, 5)
+            mx(1, Y, 5)
+            mx(3, Z, 5)
+            mx(2, Y, 5)
+            prod_w(2, 3)
+            leave(0, Y, "s")
+            tr_w(2, 0)
+            leave(2, Y, "s")
+            tr_w(2, 1)
+            prod_w(2, 5)
+            cast_w(3, 1)
+            tr_w(3, 0)
+            mx(2, Z, 2)
+            mx(0, Z, 2)
+            mx(3, Z, 0)
+            mx(2, Z, 3)
+            quant_c(1, Z)
+            mx(0, Z, 3)
+            leave(1, Y, "s")
+            prod_w(2, 0)
+            tr_w(3, 2)
+            cast_w(3, 2)
+            mx(0, Z, 4)
+            mx(3, Y, 2)
+            mx(0, Z, 5)
+            prod_w(2, 1)
+            mx(2, Z, 4)
+            mx(3, Z, 1)
+            mx(3, Y, 3)
+            leave(3, Z, "s")
+            mx(2, Z, 5)
+            mx(0, Z, 0)
+            tr_w(3, 1)
+            tr_w(3, 5)
+            quant_w(2, 0)
+            mx(2, Z, 0)
+            mx(0, Z, 1)
+            quant_w(2, 1)
+            mx(3, Y, 0)
+            mx(2, Z, 1)
+            mx(4, X, 0)
+            quant_w(2, 2)
+            leave(2, Z, "s")
+            mx(3, Y, 1)
+            leave(0, Z, "s")
+            mx(4, X, 1)
+            prod_w(3, 1)
+            store(0, 1)
+            store(0, 2)
+            mx(1, Z, 2)
+            mx(5, X, 0)
+            mx(1, Z, 3)
+            mx(4, X, 2)
+            mx(1, Z, 4)
+            mx(3, Y, 4)
+            mx(5, X, 1)
+            prod_w(3, 0)
+            mx(4, X, 3)
+            mx(3, Y, 5)
+            mx(1, Z, 5)
+            mx(4, X, 4)
+            leave(3, Y, "s")
+            prod_w(3, 2)
+            mx(1, Z, 0)
+            mx(5, X, 2)
+            mx(4, X, 5)
+            tr_w(3, 4)
+            leave(4, X, "s")
+            prod_w(3, 5)
+            tr_w(3, 3)
+            mx(5, Z, 0)
+            mx(1, Z, 1)
+            mx(4, Y, 0)
+            quant_w(3, 0)
+            mx(5, X, 3)
+            mx(5, Z, 1)
+            mx(4, Y, 1)
+            leave(1, Z, "v")
+            mx(5, Z, 2)
+            prod_w(3, 3)
+            mx(5, X, 4)
+            store(2, 1)
+            store(2, 2)
+            mx(4, Z, 0)
+            store(1, 1)
+            store(1, 2)
+            mx(7, Z, 0, "tr")
+            store(3, 1)
+            store(3, 2)
+            mx(4, Y, 2)
+            mx(5, Z, 3)
+            mx(5, X, 5)
+            mx(4, Y, 3)
+            leave(5, X, "s")
+            mx(6, Z, 0, "tr")
+            quant_w(3, 1)
+            mx(4, Z, 1)
+            mx(7, Z, 1, "tr")
+            mx(5, Z, 4)
+            mx(4, Y, 4)
+            mx(6, Z, 1, "tr")
+            prod_w(3, 4)
+            mx(4, Z, 2)
+            mx(5, Z, 5)
+            mx(7, Y, 0)
+            leave(5, Z, "s")
+            mx(4, Z, 3)
+            mx(4, Y, 5)
+            mx(6, Z, 2, "tr")
+            mx(7, Y, 1)
+            mx(7, Z, 2, "tr")
+            mx(7, X, 0)
+            leave(4, Y, "v")
+            mx(7, Y, 2)
+            mx(7, X, 1)
+            quant_w(3, 2)
+            mx(4, Z, 4)
+            mx(6, Z, 3, "tr")
+            mx(7, Y, 3)
+            mx(5, Y, 0)
+            mx(4, Z, 5)
+            mx(7, Y, 4)
+            leave(4, Z, "v")
+            mx(7, X, 2)
+            mx(6, Z, 4, "tr")
+            mx(7, Z, 3, "tr")
+            store(4, 0)
+            mx(5, Y, 1)
+            store(4, 1)
+            store(4, 2)
+            mx(7, Y, 5)
+            store(5, 0)
+            mx(7, X, 3)
+            leave(7, Y, "v")
+            mx(5, Y, 2)
+            mx(6, X, 0)
+            mx(7, X, 4)
+            mx(7, Z, 4, "tr")
+            mx(6, Y, 0)
+            mx(7, X, 5)
+            mx(6, Y, 1)
+            mx(5, Y, 3)
+            mx(6, X, 1)
+            mx(5, Y, 4)
+            mx(7, Z, 5, "tr")
+            mx(6, Y, 2)
+            leave(7, Z, "v")
+            mx(6, X, 2)
+            leave(7, X, "v")
+            mx(6, Y, 3)
+            mx(5, Y, 5)
+            mx(6, Y, 4)
+            store(7, 0)
+            store(7, 1)
+            store(7, 2)
+            leave(5, Y, "s")
+            mx(6, X, 3)
+            mx(6, Y, 5)
+            mx(6, X, 4)
+            store(5, 1)
+            store(5, 2)
+            leave(6, Y, "s")
+            mx(6, Z, 5, "tr")
+            mx(6, X, 5)
+            leave(6, Z, "v")
+            store(6, 1)
+            store(6, 2)
+            leave(6, X, "s")
+            store(6, 0)

@@ -43,7 +43,7 @@ def tile_afnb_pb_kernel(tc, context, high, ww, bw, wf_bytes, wf_scale, bfuse, gf
         ctx_t = context.rearrange("b (p t) h w -> b p t (h w)", t=4)
         high_t = high.rearrange("b (g p t) h w -> b g p t (h w)", p=P, t=4)
         wbytes, raws = {}, {}
-        wwr = keep.tile([P, GC, 4, CV], BF16, name="wwr")
+        wwr = {}
 
         def load_w(q, m, lo=0, hi=CF):
             if q not in wbytes:
@@ -51,11 +51,14 @@ def tile_afnb_pb_kernel(tc, context, high, ww, bw, wf_bytes, wf_scale, bfuse, gf
             nc.sync.dma_start(out=wbytes[q][:, m, lo:hi], in_=wf_t[q, :, m, lo:hi])
 
         def load_ww(g):
-            nc.sync.dma_start(out=wwr[:, g], in_=ww_t[g])
+            wwr[g] = rot.tile([P, 4, CV], BF16, name="wb", bufs=6)
+            nc.sync.dma_start(out=wwr[g][:], in_=ww_t[g])
 
-        def load_act(g, b):
-            raws[g, b] = rot.tile([P, 4, HW], BF16, name="raw", bufs=7)
-            nc.sync.dma_start(out=raws[g, b][:], in_=ctx_t[b] if g == CTX else high_t[b, g])
+        def load_act(g, b, lo=0, hi=HW):
+            if (g, b) not in raws:
+                raws[g, b] = rot.tile([P, 4, HW], BF16, name="raw", bufs=8)
+            src = ctx_t[b] if g == CTX else high_t[b, g]
+            nc.sync.dma_start(out=raws[g, b][:, :, lo:hi], in_=src[:, :, lo:hi])
 
         ident = keep.tile([P, P], F32, name="ident")
         rows = keep.tile([P, P], BF16, name="rows")
@@ -69,13 +72,18 @@ def tile_afnb_pb_kernel(tc, context, high, ww, bw, wf_bytes, wf_scale, bfuse, gf
         rstd = keep.tile([P, MT], F32, name="rstd")
         bdiff = keep.tile([P, MT], F32, name="bdiff")
 
+        warm_in = keep.tile([P, 512], BF16, name="warm_in")
+
         def load_consts():
+            nc.vector.memset(warm_in[:], 0.0)
+            make_identity(nc, ident[:])
             nc.gpsimd.memset(rows[:], 0.0)
             for i, v in enumerate((bfuse, gf, bef, mf, vf)):
                 nc.gpsimd.dma_start(out=rows[MT * i : MT * (i + 1), :], in_=v.rearrange("(m p) -> m p", p=P))
             nc.scalar.dma_start(out=ws[:], in_=wf_scale.rearrange("o (g p t) -> p (o g) t", p=P, t=4))
             nc.scalar.dma_start(out=bwt[:], in_=bw.rearrange("(g p t) -> p g t", p=P, t=4))
-            make_identity(nc, ident[:])
+
+        def make_consts():
             nc.gpsimd.tensor_copy(out=rows32[:], in_=rows[:])
             nc.gpsimd.memset(half[:], -0.5)
 
@@ -109,11 +117,13 @@ def tile_afnb_pb_kernel(tc, context, high, ww, bw, wf_bytes, wf_scale, bfuse, gf
 
         def inter(g, b, eng="s", lo=0, hi=HW):
             if (g, b) not in grps:
-                grps[g, b] = rot.tile([P, HW, 4], BF16, name="grp", bufs=3, align_bytes=64)
-            dst = grps[g, b][:, lo:hi, :]
-            src = raws[g, b][:, :, lo:hi].rearrange("p t n -> p n t")
+                grps[g, b] = rot.tile([P, HW, 4], BF16, name="grp", bufs=4, align_bytes=64)
+            dst = grps[g, b][:, lo:hi, :].rearrange("p (c i) t -> p c t i", i=4)
+            src = raws[g, b][:, :, lo:hi].rearrange("p t (c i) -> p c t i", i=4)
             if eng == "v":
                 nc.vector.tensor_copy(out=dst, in_=src)
+            elif eng == "g":
+                nc.gpsimd.tensor_scalar(out=dst, in0=src, scalar1=1.0, scalar2=0.0, op0=MULT, op1=ADD)
             else:
                 nc.scalar.copy(out=dst, in_=src)
 
@@ -123,27 +133,41 @@ def tile_afnb_pb_kernel(tc, context, high, ww, bw, wf_bytes, wf_scale, bfuse, gf
             quant(c, s, flat[:, 0:2048], b * HW, 512)
             quant(c, s, flat[:, 2048:2304], b * HW + 512, 64)
 
-        wwg = keep.tile([P, GC * 4, 512], BF16, name="wwg", align_bytes=64)
+        wwg = {}
         wwc = keep.tile([P, CO], U32, name="wwc", align_bytes=64)
         wwsc = keep.tile([P, CO], U8, name="wwsc", align_bytes=64)
         ww_bank = {}
 
-        def tr_ww(i):
+        def heat(bank, times):
+            for i in range(times):
+                nc.tensor.matmul(bank, lhsT=warm_in[:, 0:P], rhs=warm_in[:], start=True, stop=True)
+
+        def warm(i):
+            bank = psum.tile([P, 2, 2 * P], F32, name="tr")
+            heat(bank[:].rearrange("p u r -> p (u r)"), 1)
+
+        def tr_ww(i, warm=0):
             ww_bank[i] = psum.tile([P, 2, 2, P], F32, name="tr")
+            heat(ww_bank[i][:].rearrange("p c u r -> p (c u r)"), warm)
             for j in range(2):
                 g, t = divmod(2 * i + j, 4)
-                words = wwr[:, g, t, :].bitcast(F32)
+                words = wwr[g][:, t, :].bitcast(F32)
                 for u in range(2):
                     nc.tensor.transpose(ww_bank[i][:, j, u, :], words[:, u : CV // 2 : 2], ident[:])
 
-        def exit_ww(i):
-            nc.scalar.copy(
-                out=wwg[:, 2 * i : 2 * i + 2, :].bitcast(F32).rearrange("p c (r u) -> p c r u", u=2),
-                in_=ww_bank[i][:].rearrange("p c u r -> p c r u"),
-            )
+        def exit_ww(i, eng):
+            g, t = divmod(2 * i, 4)
+            if g not in wwg:
+                wwg[g] = rot.tile([P, 4, 512], BF16, name="wg", bufs=5, align_bytes=64)
+            dst = wwg[g][:, t : t + 2, :].bitcast(F32).rearrange("p c (r u) -> p c r u", u=2)
+            src = ww_bank[i][:].rearrange("p c u r -> p c r u")
+            if eng == "v":
+                nc.vector.tensor_copy(out=dst, in_=src)
+            else:
+                nc.scalar.copy(out=dst, in_=src)
 
         def quant_ww(g):
-            quant(wwc, wwsc, wwg[:, 4 * g : 4 * g + 4, :].rearrange("p c k -> p (c k)"), 512 * g, 512)
+            quant(wwc, wwsc, wwg[g][:].rearrange("p c k -> p (c k)"), 512 * g, 512)
 
         cgrp, cbank = {}, {}
 
@@ -160,7 +184,7 @@ def tile_afnb_pb_kernel(tc, context, high, ww, bw, wf_bytes, wf_scale, bfuse, gf
         def exit_c(g, nb):
             lo, n = X if nb < 4 else Z if nb < 5 else Y
             if (g, lo) not in cgrp:
-                cgrp[g, lo] = rot.tile([P, n, 4], BF16, name="cgrp", bufs=3, align_bytes=64)
+                cgrp[g, lo] = rot.tile([P, n, 4], BF16, name="cgrp", bufs=4, align_bytes=64)
             off = nb * P - lo
             nc.vector.tensor_tensor(
                 out=cgrp[g, lo][:, off : off + P, :], in0=cbank[g, nb][:].rearrange("p t n -> p n t"),
@@ -175,14 +199,15 @@ def tile_afnb_pb_kernel(tc, context, high, ww, bw, wf_bytes, wf_scale, bfuse, gf
         wsc = [keep.tile([P, G, 2 * P], U8, name="wsc%d" % q, align_bytes=64) for q in range(NQ)]
 
         def cast_w(q, h):
-            wb[q, h] = rot.tile([P, 2, 1024], BF16, name="wb", bufs=4)
+            wb[q, h] = rot.tile([P, 2, 1024], BF16, name="wb", bufs=6)
             for m in range(2):
                 nc.scalar.copy(out=wb[q, h][:, m], in_=wbytes[q][:, m, 1024 * h : 1024 * (h + 1)].bitcast(FP8))
 
-        def tr_w(q, g):
+        def tr_w(q, g, warm=0):
             h, j = divmod(g, 2)
             bank = psum.tile([P, 2, 2 * P], F32, name="tr")
             wbank[q, g] = bank
+            heat(bank[:].rearrange("p u r -> p (u r)"), warm)
             for m in range(2):
                 words = wb[q, h][:, m].bitcast(F32)
                 for u in range(2):
@@ -191,28 +216,12 @@ def tile_afnb_pb_kernel(tc, context, high, ww, bw, wf_bytes, wf_scale, bfuse, gf
         def prod_w(q, g):
             h, j = divmod(g, 2)
             if (q, h) not in wg:
-                wg[q, h] = rot.tile([P, 2, 1024], BF16, name="wg", bufs=3, align_bytes=64)
+                wg[q, h] = rot.tile([P, 2, 1024], BF16, name="wg", bufs=5, align_bytes=64)
             nc.vector.tensor_tensor(
                 out=wg[q, h][:, j].rearrange("p (r u e) -> p r u e", u=2, e=2),
                 in0=wbank[q, g][:].bitcast(BF16).rearrange("p u (r e) -> p r u e", e=2),
                 in1=ws[:, g, :].rearrange("p (u e) -> p u e", e=2).unsqueeze(1).to_broadcast([P, 2 * P, 2, 2]),
                 op=MULT)
-
-        planes = {}
-
-        def prod_s(q, g):
-            planes[q, g] = rot.tile([P, 4, 2 * P], BF16, name="plane", bufs=3)
-            pairs = wbank[q, g][:].bitcast(BF16)
-            for t in range(4):
-                nc.scalar.activation(out=planes[q, g][:, t, :], in_=pairs[:, t // 2, t % 2 : 4 * P : 2],
-                                     func=mybir.ActivationFunctionType.Copy, scale=ws[:, g, t : t + 1])
-
-        def inter_w(q, g):
-            h, j = divmod(g, 2)
-            if (q, h) not in wg:
-                wg[q, h] = rot.tile([P, 2, 1024], BF16, name="wg", bufs=3, align_bytes=64)
-            nc.vector.tensor_copy(out=wg[q, h][:, j].rearrange("p (r t) -> p r t", t=4),
-                                  in_=planes[q, g][:].rearrange("p t r -> p r t"))
 
         def quant_w(q, h):
             flat = wg[q, h][:].rearrange("p j k -> p (j k)")
@@ -257,375 +266,385 @@ def tile_afnb_pb_kernel(tc, context, high, ww, bw, wf_bytes, wf_scale, bfuse, gf
         load_consts()
         load_w(0, 1, 0, 1024)
         load_w(0, 0, 0, 1024)
-        load_act(CTX, 0)
-        load_w(0, 0, 1024, 2048)
+        load_act(CTX, 0, 288, 576)
+        load_act(CTX, 0, 0, 288)
         load_w(0, 1, 1024, 2048)
         load_ww(1)
+        load_w(0, 0, 1024, 2048)
+        load_ww(0)
+        load_act(0, 0)
+        load_w(0, 0, 2048, 3072)
         load_w(0, 1, 2048, 3072)
         load_act(CTX, 1)
-        load_act(0, 0)
-        load_ww(0)
-        load_w(0, 0, 2048, 3072)
         load_w(1, 1)
-        load_w(1, 0)
-        load_w(2, 0)
-        load_act(1, 0)
-        load_act(3, 1)
-        load_act(3, 0)
-        load_w(3, 1)
         load_act(2, 0)
-        load_act(0, 1)
-        load_w(2, 1)
+        load_w(1, 0)
+        load_w(3, 1)
         load_act(2, 1)
+        load_w(2, 0)
+        load_act(3, 0)
+        load_act(3, 1)
+        load_act(1, 0)
         load_act(1, 1)
+        load_act(0, 1)
         load_w(3, 0)
+        load_w(2, 1)
         with tc.manual_schedule(engines={mybir.EngineType.PE, mybir.EngineType.DVE, mybir.EngineType.Activation}):
+            warm(5)
+            warm(4)
+            warm(3)
+            warm(8)
+            warm(9)
+            warm(2)
             cast_w(0, 0)
-            inter(CTX, 0, "v", 0, 288)
-            inter(CTX, 0, "s", 288, 576)
+            inter(CTX, 0, "v", 288, 576)
+            inter(CTX, 0, "s", 0, 288)
             tr_w(0, 0)
-            tr_w(0, 1)
+            warm(16)
             prod_w(0, 0)
+            warm(13)
+            tr_w(0, 1)
             cast_w(0, 1)
-            tr_ww(3)
             prod_w(0, 1)
+            make_consts()
             tr_ww(2)
-            exit_ww(3)
-            tr_w(0, 3)
+            tr_ww(3)
+            exit_ww(2, "s")
             quant_act(CTX, 0)
-            exit_ww(2)
             tr_w(0, 2)
-            inter(CTX, 1, "s", 0, 288)
-            quant_ww(1)
-            prod_w(0, 3)
-            stage1(1, 0)
-            stage1(1, 3)
-            inter(CTX, 1, "s", 288, 576)
-            stage1(1, 2)
+            exit_ww(3, "s")
+            tr_ww(0)
+            quant_w(0, 0)
+            inter(0, 0, "s", 0, 288)
+            tr_w(0, 3)
             prod_w(0, 2)
             tr_ww(1)
-            tr_ww(0)
-            exit_ww(1)
-            exit_c(1, 0)
+            exit_ww(0, "s")
+            inter(0, 0, "v", 288, 576)
             tr_consts()
-            stage1(1, 1)
-            exit_ww(0)
-            quant_w(0, 1)
-            cast_w(1, 2)
-            quant_ww(0)
-            exit_c(1, 3)
-            stage1(0, 0)
             cast_w(0, 2)
-            quant_act(CTX, 1)
-            stage1(0, 2)
-            exit_c(1, 2)
-            cast_w(1, 1)
-            tr_w(0, 5)
+            quant_ww(1)
+            prod_w(0, 3)
+            stage1(1, 1)
+            exit_ww(1, "s")
+            inter(CTX, 1, "s", 0, 288)
+            stage1(1, 0)
+            quant_ww(0)
+            stage1(1, 2)
             exit_c(1, 1)
-            stage1(0, 3)
-            exit_c(0, 0)
-            exit_consts()
-            stage1(1, 8)
-            cast_w(1, 0)
-            consts()
-            tr_w(0, 4)
-            quant_w(0, 0)
-            stage1(0, 6)
-            exit_c(0, 2)
-            inter(0, 0, "s", 288, 576)
-            exit_c(1, 8)
+            tr_w(0, 5)
+            inter(CTX, 1, "s", 288, 576)
+            exit_c(1, 0)
+            stage1(1, 3)
+            exit_c(1, 2)
             stage1(0, 1)
-            tr_w(1, 3)
-            exit_c(0, 3)
-            inter(0, 0, "s", 0, 288)
-            tr_w(1, 5)
-            exit_c(0, 1)
-            stage1(0, 8)
-            quant_c(1, X)
-            stage1(1, 4)
-            inter(1, 0, "s", 0, 288)
-            quant_c(0, X)
-            exit_c(0, 8)
-            quant_act(0, 0)
-            inter(1, 0, "s", 288, 576)
-            exit_c(0, 6)
-            prod_w(0, 5)
-            mx(0, X, 2)
-            inter(2, 0, "s", 0, 288)
-            mx(1, X, 2)
-            prod_w(1, 3)
-            tr_w(1, 2)
-            inter(3, 0, "s", 0, 288)
-            mx(0, X, 0)
-            stage1(1, 5)
-            prod_w(0, 4)
-            mx(1, X, 0)
-            inter(3, 0, "s", 288, 576)
-            quant_act(1, 0)
+            stage1(0, 3)
+            exit_c(1, 3)
+            cast_w(1, 2)
+            stage1(0, 0)
+            quant_act(CTX, 1)
+            tr_w(0, 4)
+            cast_w(1, 1)
+            exit_c(0, 0)
             tr_w(1, 4)
-            exit_c(1, 4)
-            mx(0, X, 1)
+            exit_c(0, 1)
+            stage1(1, 5)
             inter(2, 0, "s", 288, 576)
-            mx(0, X, 3)
-            prod_w(1, 5)
-            tr_w(1, 1)
-            mx(1, X, 1)
-            quant_act(3, 0)
-            cast_w(2, 2)
-            mx(1, X, 3)
+            quant_act(0, 0)
+            stage1(1, 8)
+            exit_c(0, 3)
+            exit_c(1, 8)
+            exit_consts()
+            cast_w(1, 0)
+            stage1(0, 2)
+            consts()
+            stage1(0, 5)
+            exit_c(1, 5)
+            tr_w(1, 2)
+            quant_c(1, X)
+            inter(2, 0, "s", 0, 288)
+            stage1(0, 7)
+            prod_w(0, 4)
+            stage1(1, 7)
+            inter(1, 0, "s", 0, 288)
+            prod_w(0, 5)
+            exit_c(0, 2)
+            inter(1, 0, "s", 288, 576)
+            tr_w(1, 5)
             quant_w(0, 2)
-            tr_w(1, 0)
             quant_act(2, 0)
-            inter(1, 1, "s", 288, 576)
-            stage1(1, 6)
-            exit_c(1, 6)
-            mx(1, X, 4)
+            inter(3, 0, "s", 288, 576)
+            quant_w(0, 1)
             mx(0, X, 4)
-            prod_w(1, 2)
-            cast_w(2, 1)
+            quant_act(1, 0)
+            inter(3, 0, "s", 0, 288)
+            exit_c(0, 5)
+            mx(0, X, 3)
+            exit_c(0, 7)
+            mx(1, X, 4)
+            mx(1, X, 1)
+            cast_w(2, 0)
+            prod_w(1, 4)
+            mx(1, X, 3)
+            mx(1, X, 2)
+            tr_w(1, 3)
+            inter(1, 1, "s", 0, 288)
+            quant_act(3, 0)
+            tr_w(1, 1)
+            prod_w(1, 5)
             mx(1, X, 5)
             mx(0, X, 5)
-            prod_w(1, 4)
-            tr_w(2, 4)
-            inter(0, 1, "s", 288, 576)
-            exit_c(1, 5)
-            tr_w(2, 2)
-            leave(0, X, "s")
-            quant_w(1, 1)
-            leave(1, X, "s")
-            stage1(0, 5)
-            prod_w(1, 0)
-            inter(1, 1, "s", 0, 288)
-            stage1(1, 7)
-            mx(3, X, 2)
-            mx(2, X, 2)
-            quant_w(1, 2)
-            mx(2, X, 3)
-            prod_w(1, 1)
-            inter(0, 1, "s", 0, 288)
-            mx(3, X, 3)
-            mx(3, X, 4)
-            exit_c(0, 5)
-            tr_w(2, 3)
-            inter(2, 1, "s", 288, 576)
-            exit_c(1, 7)
-            mx(2, X, 4)
-            mx(3, X, 5)
-            quant_w(1, 0)
-            stage1(0, 7)
-            mx(2, X, 5)
-            quant_act(0, 1)
-            inter(2, 1, "s", 0, 288)
-            mx(3, X, 0)
-            mx(2, X, 0)
-            exit_c(0, 7)
-            mx(3, X, 1)
-            mx(2, X, 1)
-            quant_act(1, 1)
-            tr_w(2, 5)
-            leave(3, X, "s")
-            quant_c(1, Y)
-            leave(2, X, "s")
-            stage1(0, 4)
-            store(3, 0)
-            store(0, 0)
-            mx(0, Y, 2)
-            inter(3, 1, "s", 0, 288)
-            quant_c(0, Y)
-            mx(2, Y, 2)
-            store(2, 0)
-            store(1, 0)
-            mx(1, Y, 2)
-            exit_c(0, 4)
-            mx(0, Y, 3)
-            mx(2, Y, 3)
-            quant_act(2, 1)
-            mx(1, Y, 3)
             inter(3, 1, "s", 288, 576)
-            mx(0, Y, 0)
-            mx(2, Y, 0)
-            prod_w(2, 2)
-            mx(0, Y, 1)
-            mx(2, Y, 1)
-            mx(1, Y, 0)
-            cast_w(2, 0)
-            mx(0, Y, 4)
-            quant_act(3, 1)
-            mx(1, Y, 1)
-            mx(3, Z, 2)
-            mx(2, Y, 4)
-            quant_c(0, Z)
-            mx(3, Z, 3)
-            mx(1, Y, 4)
-            prod_w(2, 4)
-            cast_w(3, 0)
-            mx(3, Z, 4)
-            mx(0, Y, 5)
-            mx(1, Y, 5)
-            mx(3, Z, 5)
-            mx(2, Y, 5)
-            prod_w(2, 3)
-            leave(0, Y, "s")
-            tr_w(2, 0)
-            leave(2, Y, "s")
+            stage1(0, 4)
+            mx(0, X, 1)
+            prod_w(1, 2)
+            cast_w(2, 1)
+            quant_c(0, X)
+            tr_w(1, 0)
+            prod_w(1, 3)
+            mx(0, X, 0)
+            cast_w(2, 2)
+            mx(1, X, 0)
+            mx(0, X, 2)
+            exit_c(1, 7)
+            tr_w(2, 3)
+            leave(1, X, "s")
             tr_w(2, 1)
-            prod_w(2, 5)
-            cast_w(3, 1)
-            tr_w(3, 0)
-            mx(2, Z, 2)
-            mx(0, Z, 2)
-            mx(3, Z, 0)
-            mx(2, Z, 3)
-            quant_c(1, Z)
-            mx(0, Z, 3)
-            leave(1, Y, "s")
-            prod_w(2, 0)
-            tr_w(3, 2)
-            cast_w(3, 2)
-            mx(0, Z, 4)
-            mx(3, Y, 2)
-            mx(0, Z, 5)
-            prod_w(2, 1)
-            mx(2, Z, 4)
-            mx(3, Z, 1)
-            mx(3, Y, 3)
-            leave(3, Z, "s")
-            mx(2, Z, 5)
-            mx(0, Z, 0)
-            tr_w(3, 1)
-            tr_w(3, 5)
-            quant_w(2, 0)
-            mx(2, Z, 0)
-            mx(0, Z, 1)
-            quant_w(2, 1)
-            mx(3, Y, 0)
-            mx(2, Z, 1)
-            mx(4, X, 0)
-            quant_w(2, 2)
-            leave(2, Z, "s")
-            mx(3, Y, 1)
-            leave(0, Z, "s")
-            mx(4, X, 1)
-            prod_w(3, 1)
-            store(0, 1)
-            store(0, 2)
-            mx(1, Z, 2)
-            mx(5, X, 0)
-            mx(1, Z, 3)
-            mx(4, X, 2)
-            mx(1, Z, 4)
-            mx(3, Y, 4)
-            mx(5, X, 1)
-            prod_w(3, 0)
-            mx(4, X, 3)
+            quant_w(1, 1)
+            leave(0, X, "s")
+            exit_c(0, 4)
+            stage1(0, 8)
+            inter(2, 1, "s", 0, 288)
+            stage1(0, 6)
+            quant_w(1, 2)
+            prod_w(1, 1)
+            mx(3, X, 5)
+            mx(3, X, 2)
+            inter(3, 1, "s", 0, 288)
+            mx(3, X, 4)
+            mx(3, X, 3)
+            prod_w(1, 0)
+            stage1(1, 4)
+            tr_w(2, 5)
+            inter(1, 1, "s", 288, 576)
+            exit_c(0, 8)
+            tr_w(2, 0)
+            quant_w(1, 0)
+            stage1(1, 6)
+            inter(0, 1, "s", 0, 288)
+            exit_c(0, 6)
+            mx(3, X, 0)
+            mx(3, X, 1)
+            quant_act(1, 1)
+            mx(2, X, 0)
+            mx(2, X, 2)
+            quant_act(3, 1)
+            mx(2, X, 3)
+            leave(3, X, "s")
+            mx(2, X, 1)
+            mx(2, X, 4)
+            inter(0, 1, "s", 288, 576)
+            exit_c(1, 4)
+            mx(1, Y, 3)
+            mx(1, Y, 5)
+            quant_c(0, Y)
+            mx(2, X, 5)
+            mx(2, Y, 5)
+            exit_c(1, 6)
+            mx(2, Y, 3)
+            leave(2, X, "s")
+            mx(1, Y, 0)
+            quant_act(0, 1)
+            mx(2, Y, 0)
+            inter(2, 1, "s", 288, 576)
+            mx(0, Y, 5)
             mx(3, Y, 5)
-            mx(1, Z, 5)
-            mx(4, X, 4)
-            leave(3, Y, "s")
-            prod_w(3, 2)
-            mx(1, Z, 0)
-            mx(5, X, 2)
-            mx(4, X, 5)
-            tr_w(3, 4)
-            leave(4, X, "s")
-            prod_w(3, 5)
-            tr_w(3, 3)
-            mx(5, Z, 0)
+            quant_c(1, Y)
+            mx(0, Y, 0)
+            mx(3, Y, 3)
+            mx(0, Y, 3)
+            mx(1, Y, 2)
+            quant_act(2, 1)
+            mx(0, Y, 2)
+            mx(3, Y, 1)
+            prod_w(2, 3)
+            mx(0, Y, 1)
+            mx(0, Y, 4)
+            mx(1, Y, 4)
+            mx(1, Y, 1)
+            prod_w(2, 1)
+            mx(2, Y, 2)
+            leave(1, Y, "s")
+            mx(2, Y, 4)
+            mx(2, Y, 1)
+            mx(3, Y, 4)
+            quant_c(0, Z)
+            leave(2, Y, "s")
+            mx(3, Y, 0)
+            quant_c(1, Z)
+            mx(2, Z, 3)
+            prod_w(2, 0)
+            mx(3, Y, 2)
+            leave(0, Y, "s")
+            mx(2, Z, 4)
+            mx(1, Z, 2)
             mx(1, Z, 1)
-            mx(4, Y, 0)
-            quant_w(3, 0)
+            mx(2, Z, 5)
+            mx(2, Z, 1)
+            mx(2, Z, 2)
+            mx(1, Z, 0)
+            leave(3, Y, "s")
+            tr_w(2, 2)
+            prod_w(2, 5)
+            cast_w(3, 0)
+            tr_w(2, 4)
+            mx(0, Z, 4)
+            mx(3, Z, 1)
+            prod_w(2, 2)
+            mx(1, Z, 3)
+            mx(0, Z, 5)
+            mx(3, Z, 4)
+            cast_w(3, 2)
+            mx(0, Z, 0)
+            mx(1, Z, 4)
+            mx(3, Z, 0)
+            mx(1, Z, 5)
+            mx(2, Z, 0)
+            mx(3, Z, 5)
+            mx(0, Z, 1)
+            mx(3, Z, 3)
+            tr_w(3, 1)
+            leave(2, Z, "v")
+            quant_w(2, 1)
+            leave(1, Z, "s")
+            tr_w(3, 4)
+            cast_w(3, 1)
+            quant_w(2, 0)
+            tr_w(3, 5)
+            prod_w(2, 4)
+            mx(3, Z, 2)
+            mx(4, X, 3)
+            mx(5, X, 1)
+            mx(0, Z, 2)
+            mx(0, Z, 3)
+            mx(4, X, 2)
+            leave(3, Z, "v")
             mx(5, X, 3)
-            mx(5, Z, 1)
-            mx(4, Y, 1)
-            leave(1, Z, "v")
-            mx(5, Z, 2)
-            prod_w(3, 3)
-            mx(5, X, 4)
-            store(2, 1)
-            store(2, 2)
-            mx(4, Z, 0)
-            store(1, 1)
-            store(1, 2)
-            mx(7, Z, 0, "tr")
-            store(3, 1)
+            leave(0, Z, "v")
+            mx(4, X, 1)
             store(3, 2)
+            quant_w(2, 2)
+            store(1, 0)
+            store(0, 2)
+            mx(5, Y, 0)
+            store(1, 2)
+            store(0, 1)
+            store(0, 0)
+            mx(5, X, 2)
+            store(3, 0)
+            prod_w(3, 1)
+            store(2, 1)
             mx(4, Y, 2)
-            mx(5, Z, 3)
+            mx(4, X, 4)
+            mx(5, Y, 4)
+            mx(5, Y, 1)
+            prod_w(3, 4)
+            mx(4, X, 5)
+            mx(5, Y, 5)
+            mx(5, Y, 3)
+            mx(4, X, 0)
+            prod_w(3, 5)
+            mx(4, Y, 1)
+            store(3, 1)
+            tr_w(3, 0)
+            store(1, 1)
+            tr_w(3, 2)
+            leave(4, X, "v")
+            store(2, 2)
+            tr_w(3, 3)
+            prod_w(3, 0)
+            store(4, 0)
+            mx(5, X, 0)
+            mx(5, Z, 2)
+            mx(5, X, 4)
+            mx(5, Z, 1)
+            quant_w(3, 2)
+            mx(4, Y, 5)
             mx(5, X, 5)
             mx(4, Y, 3)
+            quant_w(3, 0)
             leave(5, X, "s")
-            mx(6, Z, 0, "tr")
-            quant_w(3, 1)
-            mx(4, Z, 1)
-            mx(7, Z, 1, "tr")
-            mx(5, Z, 4)
-            mx(4, Y, 4)
-            mx(6, Z, 1, "tr")
-            prod_w(3, 4)
-            mx(4, Z, 2)
-            mx(5, Z, 5)
-            mx(7, Y, 0)
-            leave(5, Z, "s")
-            mx(4, Z, 3)
-            mx(4, Y, 5)
-            mx(6, Z, 2, "tr")
-            mx(7, Y, 1)
-            mx(7, Z, 2, "tr")
-            mx(7, X, 0)
-            leave(4, Y, "v")
-            mx(7, Y, 2)
-            mx(7, X, 1)
-            quant_w(3, 2)
-            mx(4, Z, 4)
-            mx(6, Z, 3, "tr")
-            mx(7, Y, 3)
-            mx(5, Y, 0)
-            mx(4, Z, 5)
-            mx(7, Y, 4)
-            leave(4, Z, "v")
-            mx(7, X, 2)
-            mx(6, Z, 4, "tr")
-            mx(7, Z, 3, "tr")
-            store(4, 0)
-            mx(5, Y, 1)
-            store(4, 1)
-            store(4, 2)
-            mx(7, Y, 5)
-            store(5, 0)
-            mx(7, X, 3)
-            leave(7, Y, "v")
             mx(5, Y, 2)
-            mx(6, X, 0)
-            mx(7, X, 4)
-            mx(7, Z, 4, "tr")
-            mx(6, Y, 0)
-            mx(7, X, 5)
-            mx(6, Y, 1)
-            mx(5, Y, 3)
-            mx(6, X, 1)
-            mx(5, Y, 4)
-            mx(7, Z, 5, "tr")
-            mx(6, Y, 2)
-            leave(7, Z, "v")
-            mx(6, X, 2)
-            leave(7, X, "v")
-            mx(6, Y, 3)
-            mx(5, Y, 5)
-            mx(6, Y, 4)
-            store(7, 0)
-            store(7, 1)
-            store(7, 2)
+            mx(4, Y, 0)
+            prod_w(3, 2)
             leave(5, Y, "s")
-            mx(6, X, 3)
-            mx(6, Y, 5)
-            mx(6, X, 4)
+            mx(5, Z, 5)
+            mx(6, Z, 4, "tr")
+            mx(6, Z, 1, "tr")
+            mx(5, Z, 3)
+            mx(5, Z, 4)
+            mx(4, Z, 2)
+            mx(5, Z, 0)
+            mx(4, Y, 4)
+            leave(5, Z, "s")
+            mx(7, Z, 5, "tr")
+            mx(4, Z, 1)
+            prod_w(3, 3)
+            mx(4, Z, 3)
+            mx(4, Z, 5)
+            leave(4, Y, "s")
             store(5, 1)
+            mx(7, Z, 4, "tr")
             store(5, 2)
-            leave(6, Y, "s")
+            mx(6, Y, 5)
+            mx(7, Z, 1, "tr")
+            mx(6, Y, 1)
+            mx(7, Y, 1)
+            mx(7, Z, 0, "tr")
+            mx(7, Y, 4)
+            quant_w(3, 1)
+            mx(7, X, 5)
+            mx(6, Y, 0)
+            mx(4, Z, 4)
+            mx(6, Y, 4)
+            mx(6, Z, 0, "tr")
+            mx(7, Z, 3, "tr")
+            mx(6, Z, 3, "tr")
+            mx(6, Y, 2)
+            mx(6, Y, 3)
             mx(6, Z, 5, "tr")
-            mx(6, X, 5)
-            leave(6, Z, "v")
+            mx(4, Z, 0)
+            mx(6, Z, 2, "tr")
+            mx(7, X, 4)
+            leave(6, Y, "s")
+            mx(7, Y, 5)
+            mx(7, Y, 0)
+            leave(6, Z, "s")
+            leave(4, Z, "s")
+            mx(7, X, 0)
+            store(4, 1)
+            mx(7, X, 1)
             store(6, 1)
+            store(2, 0)
+            store(4, 2)
+            mx(7, Z, 2, "tr")
+            mx(6, X, 1)
+            leave(7, Z, "s")
+            mx(7, X, 3)
+            store(7, 1)
+            mx(6, X, 2)
+            store(5, 0)
             store(6, 2)
+            mx(7, Y, 2)
+            mx(7, Y, 3)
+            mx(7, X, 2)
+            leave(7, Y, "v")
+            mx(6, X, 0)
+            mx(6, X, 4)
+            mx(6, X, 3)
+            leave(7, X, "v")
+            store(7, 2)
+            mx(6, X, 5)
+            store(7, 0)
             leave(6, X, "s")
             store(6, 0)

@@ -203,15 +203,24 @@ def tile_afnb_pb_kernel(tc, context, high, ww, bw, wf_bytes, wf_scale, bfuse, gf
             for m in range(2):
                 nc.scalar.copy(out=wb[q, h][:, m], in_=wbytes[q][:, m, 1024 * h : 1024 * (h + 1)].bitcast(FP8))
 
+        wp = {}
+
+        def perm_w(q, h):
+            wp[q, h] = rot.tile([P, 2, 1024], BF16, name="wb", bufs=6)
+            nc.scalar.copy(
+                out=wp[q, h][:].rearrange("p m k -> p (m k)").bitcast(F32).rearrange("p (g u w) -> p g u w", u=2, w=P),
+                in_=wb[q, h][:].rearrange("p m k -> p (m k)").bitcast(F32).rearrange("p (g w u) -> p g u w", u=2, w=P))
+
         def tr_w(q, g, warm=0):
             h, j = divmod(g, 2)
             bank = psum.tile([P, 2, 2 * P], F32, name="tr")
             wbank[q, g] = bank
             heat(bank[:].rearrange("p u r -> p (u r)"), warm)
             for m in range(2):
-                words = wb[q, h][:, m].bitcast(F32)
+                words = (wp if (q, h) in wp else wb)[q, h][:, m].bitcast(F32)
                 for u in range(2):
-                    nc.tensor.transpose(bank[:, u, m * P : (m + 1) * P], words[:, 256 * j + u : 256 * (j + 1) : 2], ident[:])
+                    cols = slice(256 * j + P * u, 256 * j + P * (u + 1)) if (q, h) in wp else slice(256 * j + u, 256 * (j + 1), 2)
+                    nc.tensor.transpose(bank[:, u, m * P : (m + 1) * P], words[:, cols], ident[:])
 
         def prod_w(q, g):
             h, j = divmod(g, 2)
@@ -266,385 +275,393 @@ def tile_afnb_pb_kernel(tc, context, high, ww, bw, wf_bytes, wf_scale, bfuse, gf
         load_consts()
         load_w(0, 1, 0, 1024)
         load_w(0, 0, 0, 1024)
-        load_act(CTX, 0, 288, 576)
-        load_act(CTX, 0, 0, 288)
-        load_w(0, 1, 1024, 2048)
-        load_ww(1)
-        load_w(0, 0, 1024, 2048)
-        load_ww(0)
-        load_act(0, 0)
-        load_w(0, 0, 2048, 3072)
         load_w(0, 1, 2048, 3072)
+        load_w(0, 0, 2048, 3072)
+        load_act(CTX, 0, 288, 576)
         load_act(CTX, 1)
-        load_w(1, 1)
-        load_act(2, 0)
+        load_ww(1)
+        load_w(0, 1, 1024, 2048)
+        load_ww(0)
+        load_w(0, 0, 1024, 2048)
+        load_act(CTX, 0, 0, 288)
         load_w(1, 0)
-        load_w(3, 1)
-        load_act(2, 1)
-        load_w(2, 0)
+        load_w(1, 1)
         load_act(3, 0)
-        load_act(3, 1)
-        load_act(1, 0)
-        load_act(1, 1)
         load_act(0, 1)
-        load_w(3, 0)
+        load_act(2, 0)
+        load_w(2, 0)
         load_w(2, 1)
+        load_act(0, 0)
+        load_act(3, 1)
+        load_w(3, 1)
+        load_act(1, 0)
+        load_act(2, 1)
+        load_act(1, 1)
+        load_w(3, 0)
         with tc.manual_schedule(engines={mybir.EngineType.PE, mybir.EngineType.DVE, mybir.EngineType.Activation}):
-            warm(5)
-            warm(4)
             warm(3)
-            warm(8)
             warm(9)
-            warm(2)
+            warm(17)
+            warm(8)
+            warm(6)
+            warm(10)
             cast_w(0, 0)
-            inter(CTX, 0, "v", 288, 576)
-            inter(CTX, 0, "s", 0, 288)
-            tr_w(0, 0)
-            warm(16)
-            prod_w(0, 0)
-            warm(13)
-            tr_w(0, 1)
-            cast_w(0, 1)
-            prod_w(0, 1)
-            make_consts()
-            tr_ww(2)
-            tr_ww(3)
-            exit_ww(2, "s")
-            quant_act(CTX, 0)
-            tr_w(0, 2)
-            exit_ww(3, "s")
-            tr_ww(0)
-            quant_w(0, 0)
-            inter(0, 0, "s", 0, 288)
-            tr_w(0, 3)
-            prod_w(0, 2)
-            tr_ww(1)
-            exit_ww(0, "s")
-            inter(0, 0, "v", 288, 576)
-            tr_consts()
             cast_w(0, 2)
-            quant_ww(1)
-            prod_w(0, 3)
-            stage1(1, 1)
-            exit_ww(1, "s")
+            inter(CTX, 0, "v", 288, 576)
+            tr_w(0, 1)
+            warm(18)
+            prod_w(0, 1)
+            warm(0)
+            tr_w(0, 4)
             inter(CTX, 1, "s", 0, 288)
-            stage1(1, 0)
-            quant_ww(0)
-            stage1(1, 2)
-            exit_c(1, 1)
+            prod_w(0, 4)
+            make_consts()
+            tr_w(0, 0)
             tr_w(0, 5)
             inter(CTX, 1, "s", 288, 576)
-            exit_c(1, 0)
-            stage1(1, 3)
-            exit_c(1, 2)
-            stage1(0, 1)
-            stage1(0, 3)
-            exit_c(1, 3)
-            cast_w(1, 2)
-            stage1(0, 0)
-            quant_act(CTX, 1)
-            tr_w(0, 4)
-            cast_w(1, 1)
-            exit_c(0, 0)
-            tr_w(1, 4)
-            exit_c(0, 1)
-            stage1(1, 5)
-            inter(2, 0, "s", 288, 576)
-            quant_act(0, 0)
-            stage1(1, 8)
-            exit_c(0, 3)
-            exit_c(1, 8)
-            exit_consts()
-            cast_w(1, 0)
-            stage1(0, 2)
-            consts()
-            stage1(0, 5)
-            exit_c(1, 5)
-            tr_w(1, 2)
-            quant_c(1, X)
-            inter(2, 0, "s", 0, 288)
-            stage1(0, 7)
-            prod_w(0, 4)
-            stage1(1, 7)
-            inter(1, 0, "s", 0, 288)
+            prod_w(0, 0)
+            tr_ww(3)
+            tr_ww(2)
+            cast_w(0, 1)
             prod_w(0, 5)
-            exit_c(0, 2)
-            inter(1, 0, "s", 288, 576)
-            tr_w(1, 5)
-            quant_w(0, 2)
-            quant_act(2, 0)
-            inter(3, 0, "s", 288, 576)
-            quant_w(0, 1)
-            mx(0, X, 4)
-            quant_act(1, 0)
+            tr_ww(1)
+            exit_ww(3, "s")
+            inter(CTX, 0, "v", 0, 288)
+            tr_ww(0)
+            exit_ww(2, "s")
+            quant_w(0, 0)
+            cast_w(1, 2)
+            warm(12)
+            quant_ww(1)
+            quant_act(CTX, 0)
+            exit_ww(0, "s")
+            exit_ww(1, "s")
+            quant_act(CTX, 1)
+            stage1(1, 0)
             inter(3, 0, "s", 0, 288)
-            exit_c(0, 5)
-            mx(0, X, 3)
-            exit_c(0, 7)
-            mx(1, X, 4)
-            mx(1, X, 1)
-            cast_w(2, 0)
-            prod_w(1, 4)
-            mx(1, X, 3)
-            mx(1, X, 2)
-            tr_w(1, 3)
-            inter(1, 1, "s", 0, 288)
-            quant_act(3, 0)
-            tr_w(1, 1)
-            prod_w(1, 5)
-            mx(1, X, 5)
-            mx(0, X, 5)
-            inter(3, 1, "s", 288, 576)
+            quant_ww(0)
+            stage1(1, 2)
+            exit_c(1, 0)
+            stage1(0, 0)
+            stage1(1, 1)
+            exit_c(1, 2)
+            inter(2, 0, "s", 288, 576)
             stage1(0, 4)
-            mx(0, X, 1)
-            prod_w(1, 2)
-            cast_w(2, 1)
-            quant_c(0, X)
-            tr_w(1, 0)
-            prod_w(1, 3)
-            mx(0, X, 0)
-            cast_w(2, 2)
-            mx(1, X, 0)
-            mx(0, X, 2)
-            exit_c(1, 7)
-            tr_w(2, 3)
-            leave(1, X, "s")
-            tr_w(2, 1)
-            quant_w(1, 1)
-            leave(0, X, "s")
+            quant_w(0, 2)
+            tr_w(1, 4)
+            exit_c(0, 0)
+            tr_consts()
+            tr_w(0, 2)
+            inter(3, 0, "s", 288, 576)
+            prod_w(1, 4)
+            stage1(0, 7)
+            stage1(0, 2)
+            exit_c(1, 1)
+            cast_w(1, 0)
             exit_c(0, 4)
-            stage1(0, 8)
-            inter(2, 1, "s", 0, 288)
+            stage1(0, 3)
+            exit_consts()
+            prod_w(0, 2)
+            inter(2, 0, "s", 0, 288)
+            stage1(0, 1)
+            consts()
+            tr_w(0, 3)
+            tr_w(1, 5)
+            exit_c(0, 7)
+            cast_w(1, 1)
+            exit_c(0, 2)
+            stage1(1, 3)
+            tr_w(1, 0)
+            exit_c(0, 3)
+            inter(0, 0, "s", 288, 576)
+            quant_act(2, 0)
+            stage1(1, 7)
+            tr_w(1, 3)
+            exit_c(0, 1)
             stage1(0, 6)
-            quant_w(1, 2)
-            prod_w(1, 1)
-            mx(3, X, 5)
-            mx(3, X, 2)
-            inter(3, 1, "s", 0, 288)
-            mx(3, X, 4)
-            mx(3, X, 3)
+            cast_w(2, 0)
+            exit_c(1, 3)
+            mx(1, X, 4)
+            prod_w(1, 5)
+            cast_w(2, 2)
+            prod_w(0, 3)
+            inter(0, 0, "s", 0, 288)
+            quant_act(3, 0)
+            warm(19)
+            tr_w(1, 1)
+            inter(1, 0, "s", 0, 288)
+            quant_c(1, X)
+            mx(1, X, 5)
+            quant_w(0, 1)
+            mx(0, X, 5)
+            quant_act(0, 0)
+            inter(1, 0, "s", 288, 576)
             prod_w(1, 0)
-            stage1(1, 4)
-            tr_w(2, 5)
-            inter(1, 1, "s", 288, 576)
-            exit_c(0, 8)
-            tr_w(2, 0)
-            quant_w(1, 0)
-            stage1(1, 6)
+            perm_w(2, 0)
+            quant_act(1, 0)
+            tr_w(1, 2)
+            quant_c(0, X)
+            mx(0, X, 4)
             inter(0, 1, "s", 0, 288)
+            mx(0, X, 1)
+            mx(1, X, 1)
+            exit_c(1, 7)
+            prod_w(1, 2)
+            stage1(0, 8)
+            inter(0, 1, "s", 288, 576)
+            mx(1, X, 0)
+            mx(0, X, 0)
+            mx(0, X, 3)
+            prod_w(1, 3)
+            mx(1, X, 2)
+            inter(2, 1, "s", 288, 576)
             exit_c(0, 6)
+            tr_w(2, 1)
+            tr_w(2, 0)
+            exit_c(0, 8)
+            mx(0, X, 2)
+            perm_w(2, 2)
+            mx(1, X, 3)
+            prod_w(1, 1)
+            stage1(1, 6)
+            leave(1, X, "s")
+            quant_w(1, 1)
+            tr_w(2, 5)
+            leave(0, X, "s")
+            store(1, 0)
+            tr_w(2, 4)
+            quant_w(1, 2)
+            inter(1, 1, "s", 288, 576)
+            stage1(0, 5)
+            mx(3, X, 3)
+            quant_w(1, 0)
+            mx(3, X, 4)
+            stage1(1, 5)
+            exit_c(1, 6)
             mx(3, X, 0)
+            inter(1, 1, "s", 0, 288)
+            mx(3, X, 2)
+            exit_c(0, 5)
+            stage1(1, 8)
+            mx(3, X, 5)
+            exit_c(1, 5)
             mx(3, X, 1)
+            mx(2, X, 3)
+            exit_c(1, 8)
+            leave(3, X, "s")
+            mx(2, X, 5)
+            mx(2, X, 1)
             quant_act(1, 1)
             mx(2, X, 0)
-            mx(2, X, 2)
-            quant_act(3, 1)
-            mx(2, X, 3)
-            leave(3, X, "s")
-            mx(2, X, 1)
+            inter(2, 1, "s", 0, 288)
+            stage1(1, 4)
             mx(2, X, 4)
-            inter(0, 1, "s", 288, 576)
-            exit_c(1, 4)
-            mx(1, Y, 3)
-            mx(1, Y, 5)
-            quant_c(0, Y)
-            mx(2, X, 5)
-            mx(2, Y, 5)
-            exit_c(1, 6)
-            mx(2, Y, 3)
-            leave(2, X, "s")
-            mx(1, Y, 0)
-            quant_act(0, 1)
-            mx(2, Y, 0)
-            inter(2, 1, "s", 288, 576)
-            mx(0, Y, 5)
-            mx(3, Y, 5)
             quant_c(1, Y)
-            mx(0, Y, 0)
+            mx(2, X, 2)
             mx(3, Y, 3)
-            mx(0, Y, 3)
-            mx(1, Y, 2)
-            quant_act(2, 1)
-            mx(0, Y, 2)
+            quant_c(0, Y)
+            mx(1, Y, 3)
+            leave(2, X, "s")
             mx(3, Y, 1)
-            prod_w(2, 3)
-            mx(0, Y, 1)
-            mx(0, Y, 4)
-            mx(1, Y, 4)
-            mx(1, Y, 1)
-            prod_w(2, 1)
-            mx(2, Y, 2)
-            leave(1, Y, "s")
-            mx(2, Y, 4)
-            mx(2, Y, 1)
-            mx(3, Y, 4)
-            quant_c(0, Z)
-            leave(2, Y, "s")
+            quant_act(2, 1)
+            inter(3, 1, "s", 0, 288)
             mx(3, Y, 0)
-            quant_c(1, Z)
-            mx(2, Z, 3)
-            prod_w(2, 0)
+            mx(0, Y, 0)
+            inter(3, 1, "v", 288, 576)
+            mx(1, Y, 0)
+            mx(0, Y, 3)
+            mx(1, Y, 4)
+            quant_act(0, 1)
+            mx(1, Y, 1)
+            cast_w(2, 1)
+            mx(0, Y, 1)
+            mx(3, Y, 4)
+            quant_act(3, 1)
+            mx(1, Y, 2)
             mx(3, Y, 2)
-            leave(0, Y, "s")
-            mx(2, Z, 4)
-            mx(1, Z, 2)
-            mx(1, Z, 1)
-            mx(2, Z, 5)
-            mx(2, Z, 1)
-            mx(2, Z, 2)
-            mx(1, Z, 0)
-            leave(3, Y, "s")
-            tr_w(2, 2)
-            prod_w(2, 5)
-            cast_w(3, 0)
-            tr_w(2, 4)
-            mx(0, Z, 4)
-            mx(3, Z, 1)
-            prod_w(2, 2)
-            mx(1, Z, 3)
-            mx(0, Z, 5)
-            mx(3, Z, 4)
             cast_w(3, 2)
+            exit_c(1, 4)
+            mx(0, Y, 2)
+            mx(3, Y, 5)
+            prod_w(2, 1)
+            mx(1, Y, 5)
+            mx(2, Y, 2)
+            leave(3, Y, "s")
+            mx(0, Y, 4)
+            mx(2, Y, 1)
+            leave(1, Y, "s")
+            quant_c(0, Z)
+            mx(2, Y, 4)
+            quant_c(1, Z)
+            mx(2, Y, 0)
+            prod_w(2, 0)
+            perm_w(2, 1)
             mx(0, Z, 0)
-            mx(1, Z, 4)
-            mx(3, Z, 0)
-            mx(1, Z, 5)
-            mx(2, Z, 0)
-            mx(3, Z, 5)
-            mx(0, Z, 1)
-            mx(3, Z, 3)
-            tr_w(3, 1)
-            leave(2, Z, "v")
-            quant_w(2, 1)
-            leave(1, Z, "s")
-            tr_w(3, 4)
-            cast_w(3, 1)
-            quant_w(2, 0)
-            tr_w(3, 5)
-            prod_w(2, 4)
-            mx(3, Z, 2)
-            mx(4, X, 3)
-            mx(5, X, 1)
+            mx(1, Z, 0)
+            mx(1, Z, 2)
             mx(0, Z, 2)
+            mx(1, Z, 4)
             mx(0, Z, 3)
-            mx(4, X, 2)
-            leave(3, Z, "v")
-            mx(5, X, 3)
+            mx(2, Y, 5)
+            mx(0, Y, 5)
+            prod_w(2, 5)
+            perm_w(3, 2)
+            mx(0, Z, 5)
+            mx(0, Z, 1)
+            mx(1, Z, 5)
+            mx(1, Z, 1)
+            mx(0, Z, 4)
+            mx(1, Z, 3)
+            mx(2, Y, 3)
+            tr_w(2, 2)
+            leave(0, Y, "s")
             leave(0, Z, "v")
-            mx(4, X, 1)
-            store(3, 2)
-            quant_w(2, 2)
-            store(1, 0)
-            store(0, 2)
-            mx(5, Y, 0)
+            tr_w(2, 3)
+            quant_w(2, 0)
+            tr_w(3, 4)
+            leave(2, Y, "s")
+            prod_w(2, 4)
+            mx(3, Z, 3)
+            mx(3, Z, 4)
+            mx(3, Z, 2)
+            leave(1, Z, "s")
+            mx(3, Z, 1)
+            mx(3, Z, 0)
+            cast_w(3, 1)
+            mx(2, Z, 4)
+            mx(2, Z, 3)
             store(1, 2)
-            store(0, 1)
-            store(0, 0)
-            mx(5, X, 2)
-            store(3, 0)
-            prod_w(3, 1)
-            store(2, 1)
-            mx(4, Y, 2)
-            mx(4, X, 4)
-            mx(5, Y, 4)
-            mx(5, Y, 1)
-            prod_w(3, 4)
-            mx(4, X, 5)
-            mx(5, Y, 5)
-            mx(5, Y, 3)
-            mx(4, X, 0)
-            prod_w(3, 5)
+            mx(5, X, 1)
+            mx(2, Z, 2)
+            mx(3, Z, 5)
+            mx(2, Z, 1)
+            prod_w(2, 2)
             mx(4, Y, 1)
-            store(3, 1)
-            tr_w(3, 0)
-            store(1, 1)
-            tr_w(3, 2)
-            leave(4, X, "v")
-            store(2, 2)
-            tr_w(3, 3)
-            prod_w(3, 0)
-            store(4, 0)
+            mx(2, Z, 5)
             mx(5, X, 0)
-            mx(5, Z, 2)
-            mx(5, X, 4)
-            mx(5, Z, 1)
-            quant_w(3, 2)
-            mx(4, Y, 5)
-            mx(5, X, 5)
-            mx(4, Y, 3)
-            quant_w(3, 0)
-            leave(5, X, "s")
-            mx(5, Y, 2)
+            leave(3, Z, "s")
+            perm_w(3, 1)
             mx(4, Y, 0)
+            store(3, 1)
+            mx(2, Z, 0)
+            mx(5, Y, 1)
+            prod_w(2, 3)
+            mx(5, Y, 0)
+            tr_w(3, 5)
+            leave(2, Z, "s")
+            cast_w(3, 0)
+            tr_w(3, 3)
+            store(2, 2)
+            store(0, 0)
+            quant_w(2, 2)
+            store(0, 2)
+            store(2, 0)
+            tr_w(3, 2)
+            store(3, 2)
+            store(3, 0)
+            store(1, 1)
+            mx(4, X, 0)
+            quant_w(2, 1)
+            mx(5, X, 4)
+            store(0, 1)
+            mx(5, Y, 4)
+            prod_w(3, 5)
+            mx(4, X, 5)
+            mx(5, X, 3)
+            mx(5, X, 2)
+            mx(5, X, 5)
             prod_w(3, 2)
-            leave(5, Y, "s")
-            mx(5, Z, 5)
-            mx(6, Z, 4, "tr")
-            mx(6, Z, 1, "tr")
-            mx(5, Z, 3)
-            mx(5, Z, 4)
-            mx(4, Z, 2)
-            mx(5, Z, 0)
+            mx(4, Y, 5)
+            leave(5, X, "s")
+            mx(4, Y, 3)
+            mx(4, X, 2)
+            perm_w(3, 0)
+            mx(4, X, 1)
+            prod_w(3, 4)
             mx(4, Y, 4)
-            leave(5, Z, "s")
-            mx(7, Z, 5, "tr")
-            mx(4, Z, 1)
+            mx(4, Y, 2)
+            mx(5, Y, 5)
+            mx(4, Z, 0)
+            mx(4, X, 3)
             prod_w(3, 3)
-            mx(4, Z, 3)
+            mx(4, Z, 2)
             mx(4, Z, 5)
+            mx(5, Y, 3)
             leave(4, Y, "s")
-            store(5, 1)
-            mx(7, Z, 4, "tr")
-            store(5, 2)
-            mx(6, Y, 5)
-            mx(7, Z, 1, "tr")
-            mx(6, Y, 1)
-            mx(7, Y, 1)
-            mx(7, Z, 0, "tr")
-            mx(7, Y, 4)
-            quant_w(3, 1)
-            mx(7, X, 5)
-            mx(6, Y, 0)
+            mx(5, Y, 2)
             mx(4, Z, 4)
-            mx(6, Y, 4)
-            mx(6, Z, 0, "tr")
+            mx(4, X, 4)
+            quant_w(3, 2)
+            leave(5, Y, "s")
+            tr_w(3, 1)
+            tr_w(3, 0)
+            quant_w(3, 1)
+            leave(4, X, "s")
+            mx(4, Z, 1)
+            mx(6, Z, 4, "tr")
+            mx(5, Z, 3)
+            prod_w(3, 1)
+            mx(5, Z, 4)
+            mx(4, Z, 3)
+            mx(5, Z, 1)
+            mx(7, Z, 2, "tr")
+            mx(6, X, 5)
+            leave(4, Z, "s")
+            mx(5, Z, 5)
+            mx(5, Z, 0)
+            store(4, 2)
             mx(7, Z, 3, "tr")
-            mx(6, Z, 3, "tr")
-            mx(6, Y, 2)
+            store(4, 0)
+            mx(6, X, 3)
+            store(5, 0)
+            store(2, 1)
+            prod_w(3, 0)
+            mx(6, X, 4)
             mx(6, Y, 3)
             mx(6, Z, 5, "tr")
-            mx(4, Z, 0)
             mx(6, Z, 2, "tr")
-            mx(7, X, 4)
-            leave(6, Y, "s")
+            mx(7, Y, 4)
+            mx(6, Z, 3, "tr")
+            mx(7, Z, 4, "tr")
+            mx(6, Y, 5)
+            quant_w(3, 0)
+            mx(6, Y, 2)
+            mx(6, X, 2)
+            mx(5, Z, 2)
+            mx(7, Y, 3)
+            leave(5, Z, "v")
+            mx(6, Z, 1, "tr")
+            mx(7, Z, 5, "tr")
+            mx(6, X, 0)
+            mx(6, X, 1)
+            mx(7, Y, 2)
+            mx(7, Z, 0, "tr")
+            mx(7, Z, 1, "tr")
+            mx(6, Y, 0)
+            leave(7, Z, "v")
+            mx(6, Z, 0, "tr")
+            mx(7, X, 3)
+            leave(6, X, "v")
+            leave(6, Z, "s")
+            mx(7, X, 1)
+            mx(6, Y, 4)
+            mx(6, Y, 1)
+            store(6, 0)
+            store(5, 1)
+            store(7, 1)
+            mx(7, Y, 1)
+            store(5, 2)
+            leave(6, Y, "v")
             mx(7, Y, 5)
             mx(7, Y, 0)
-            leave(6, Z, "s")
-            leave(4, Z, "s")
-            mx(7, X, 0)
-            store(4, 1)
-            mx(7, X, 1)
-            store(6, 1)
-            store(2, 0)
-            store(4, 2)
-            mx(7, Z, 2, "tr")
-            mx(6, X, 1)
-            leave(7, Z, "s")
-            mx(7, X, 3)
-            store(7, 1)
-            mx(6, X, 2)
-            store(5, 0)
+            mx(7, X, 4)
             store(6, 2)
-            mx(7, Y, 2)
-            mx(7, Y, 3)
-            mx(7, X, 2)
             leave(7, Y, "v")
-            mx(6, X, 0)
-            mx(6, X, 4)
-            mx(6, X, 3)
-            leave(7, X, "v")
+            store(4, 1)
+            mx(7, X, 2)
+            store(6, 1)
+            mx(7, X, 5)
+            mx(7, X, 0)
             store(7, 2)
-            mx(6, X, 5)
+            leave(7, X, "s")
             store(7, 0)
-            leave(6, X, "s")
-            store(6, 0)

@@ -273,395 +273,396 @@ def tile_afnb_pb_kernel(tc, context, high, ww, bw, wf_bytes, wf_scale, bfuse, gf
                 nc.sync.dma_start(out=out_v[m, 1], in_=outs[m, 1][:, 64:640])
 
         load_consts()
-        load_w(0, 1, 0, 1024)
         load_w(0, 0, 0, 1024)
-        load_w(0, 1, 2048, 3072)
+        load_w(0, 1, 0, 1024)
         load_w(0, 0, 2048, 3072)
+        load_w(0, 1, 2048, 3072)
         load_act(CTX, 0, 288, 576)
         load_act(CTX, 1)
-        load_ww(1)
         load_w(0, 1, 1024, 2048)
-        load_ww(0)
-        load_w(0, 0, 1024, 2048)
         load_act(CTX, 0, 0, 288)
+        load_w(0, 0, 1024, 2048)
+        load_ww(1)
+        load_act(3, 0)
         load_w(1, 0)
         load_w(1, 1)
-        load_act(3, 0)
-        load_act(0, 1)
-        load_act(2, 0)
-        load_w(2, 0)
-        load_w(2, 1)
+        load_ww(0)
         load_act(0, 0)
+        load_act(2, 0)
+        load_w(2, 1)
         load_act(3, 1)
-        load_w(3, 1)
+        load_act(0, 1)
+        load_w(2, 0)
         load_act(1, 0)
-        load_act(2, 1)
         load_act(1, 1)
         load_w(3, 0)
+        load_act(2, 1)
+        load_w(3, 1)
         with tc.manual_schedule(engines={mybir.EngineType.PE, mybir.EngineType.DVE, mybir.EngineType.Activation}):
-            warm(3)
-            warm(9)
-            warm(17)
-            warm(8)
+            warm(1)
+            warm(4)
+            warm(12)
+            warm(15)
             warm(6)
-            warm(10)
+            warm(8)
             cast_w(0, 0)
+            warm(19)
             cast_w(0, 2)
             inter(CTX, 0, "v", 288, 576)
-            tr_w(0, 1)
-            warm(18)
-            prod_w(0, 1)
-            warm(0)
-            tr_w(0, 4)
-            inter(CTX, 1, "s", 0, 288)
-            prod_w(0, 4)
-            make_consts()
             tr_w(0, 0)
-            tr_w(0, 5)
-            inter(CTX, 1, "s", 288, 576)
+            tr_w(0, 1)
             prod_w(0, 0)
+            warm(23)
+            inter(CTX, 1, "s", 0, 288)
+            warm(2)
+            prod_w(0, 1)
+            make_consts()
+            tr_w(0, 4)
+            inter(CTX, 0, "s", 0, 288)
+            inter(CTX, 1, "v", 288, 576)
             tr_ww(3)
+            prod_w(0, 4)
             tr_ww(2)
             cast_w(0, 1)
-            prod_w(0, 5)
-            tr_ww(1)
-            exit_ww(3, "s")
-            inter(CTX, 0, "v", 0, 288)
-            tr_ww(0)
-            exit_ww(2, "s")
-            quant_w(0, 0)
-            cast_w(1, 2)
-            warm(12)
-            quant_ww(1)
+            tr_w(0, 5)
             quant_act(CTX, 0)
-            exit_ww(0, "s")
-            exit_ww(1, "s")
-            quant_act(CTX, 1)
-            stage1(1, 0)
-            inter(3, 0, "s", 0, 288)
-            quant_ww(0)
-            stage1(1, 2)
-            exit_c(1, 0)
-            stage1(0, 0)
-            stage1(1, 1)
-            exit_c(1, 2)
-            inter(2, 0, "s", 288, 576)
-            stage1(0, 4)
-            quant_w(0, 2)
-            tr_w(1, 4)
-            exit_c(0, 0)
-            tr_consts()
-            tr_w(0, 2)
-            inter(3, 0, "s", 288, 576)
-            prod_w(1, 4)
-            stage1(0, 7)
-            stage1(0, 2)
-            exit_c(1, 1)
-            cast_w(1, 0)
-            exit_c(0, 4)
-            stage1(0, 3)
-            exit_consts()
-            prod_w(0, 2)
-            inter(2, 0, "s", 0, 288)
-            stage1(0, 1)
-            consts()
+            exit_ww(3, "s")
             tr_w(0, 3)
-            tr_w(1, 5)
-            exit_c(0, 7)
+            quant_w(0, 0)
+            exit_ww(2, "s")
+            quant_act(CTX, 1)
+            inter(3, 0, "s", 0, 288)
+            tr_w(0, 2)
+            quant_ww(1)
+            prod_w(0, 5)
             cast_w(1, 1)
-            exit_c(0, 2)
             stage1(1, 3)
-            tr_w(1, 0)
-            exit_c(0, 3)
-            inter(0, 0, "s", 288, 576)
-            quant_act(2, 0)
-            stage1(1, 7)
-            tr_w(1, 3)
-            exit_c(0, 1)
-            stage1(0, 6)
-            cast_w(2, 0)
-            exit_c(1, 3)
-            mx(1, X, 4)
-            prod_w(1, 5)
-            cast_w(2, 2)
+            stage1(1, 0)
             prod_w(0, 3)
+            cast_w(1, 2)
+            tr_ww(0)
+            tr_w(1, 3)
+            prod_w(0, 2)
+            cast_w(1, 0)
+            stage1(1, 6)
+            stage1(1, 2)
+            quant_w(0, 2)
+            exit_ww(0, "s")
+            exit_c(1, 3)
             inter(0, 0, "s", 0, 288)
-            quant_act(3, 0)
-            warm(19)
-            tr_w(1, 1)
-            inter(1, 0, "s", 0, 288)
-            quant_c(1, X)
-            mx(1, X, 5)
+            exit_c(1, 6)
+            stage1(1, 4)
+            tr_ww(1)
+            exit_c(1, 0)
+            inter(3, 0, "s", 288, 576)
+            warm(16)
+            prod_w(1, 3)
+            stage1(1, 1)
             quant_w(0, 1)
-            mx(0, X, 5)
-            quant_act(0, 0)
+            exit_ww(1, "s")
+            tr_consts()
+            stage1(1, 8)
+            exit_c(1, 2)
+            inter(0, 0, "s", 288, 576)
+            quant_ww(0)
+            stage1(1, 5)
+            warm(21)
+            exit_c(1, 4)
+            exit_consts()
+            inter(2, 0, "s", 288, 576)
+            consts()
+            exit_c(1, 1)
+            stage1(0, 3)
+            tr_w(1, 5)
+            exit_c(1, 5)
+            inter(2, 0, "s", 0, 288)
+            exit_c(1, 8)
+            stage1(0, 2)
+            exit_c(0, 3)
+            stage1(0, 8)
+            stage1(0, 1)
+            quant_c(1, X)
+            stage1(0, 7)
             inter(1, 0, "s", 288, 576)
-            prod_w(1, 0)
-            perm_w(2, 0)
-            quant_act(1, 0)
+            tr_w(1, 4)
+            exit_c(0, 1)
             tr_w(1, 2)
-            quant_c(0, X)
-            mx(0, X, 4)
-            inter(0, 1, "s", 0, 288)
-            mx(0, X, 1)
+            exit_c(0, 2)
+            cast_w(2, 2)
+            quant_act(3, 0)
+            stage1(1, 7)
+            exit_c(0, 8)
+            inter(1, 0, "s", 0, 288)
+            exit_c(0, 7)
+            stage1(0, 0)
+            prod_w(1, 5)
+            mx(0, X, 5)
+            cast_w(2, 1)
+            tr_w(1, 1)
+            quant_act(0, 0)
+            inter(0, 1, "s", 288, 576)
+            quant_act(2, 0)
             mx(1, X, 1)
+            mx(0, X, 1)
+            mx(0, X, 2)
+            exit_c(0, 0)
+            mx(0, X, 4)
+            perm_w(2, 2)
+            quant_act(1, 0)
+            quant_c(0, X)
+            mx(0, X, 3)
+            inter(1, 1, "s", 0, 288)
+            mx(1, X, 5)
             exit_c(1, 7)
             prod_w(1, 2)
-            stage1(0, 8)
-            inter(0, 1, "s", 288, 576)
-            mx(1, X, 0)
-            mx(0, X, 0)
-            mx(0, X, 3)
-            prod_w(1, 3)
-            mx(1, X, 2)
-            inter(2, 1, "s", 288, 576)
-            exit_c(0, 6)
-            tr_w(2, 1)
-            tr_w(2, 0)
-            exit_c(0, 8)
-            mx(0, X, 2)
-            perm_w(2, 2)
-            mx(1, X, 3)
-            prod_w(1, 1)
-            stage1(1, 6)
-            leave(1, X, "s")
-            quant_w(1, 1)
-            tr_w(2, 5)
-            leave(0, X, "s")
-            store(1, 0)
-            tr_w(2, 4)
-            quant_w(1, 2)
-            inter(1, 1, "s", 288, 576)
             stage1(0, 5)
-            mx(3, X, 3)
-            quant_w(1, 0)
-            mx(3, X, 4)
-            stage1(1, 5)
-            exit_c(1, 6)
-            mx(3, X, 0)
-            inter(1, 1, "s", 0, 288)
-            mx(3, X, 2)
-            exit_c(0, 5)
-            stage1(1, 8)
-            mx(3, X, 5)
-            exit_c(1, 5)
-            mx(3, X, 1)
-            mx(2, X, 3)
-            exit_c(1, 8)
-            leave(3, X, "s")
-            mx(2, X, 5)
-            mx(2, X, 1)
-            quant_act(1, 1)
-            mx(2, X, 0)
-            inter(2, 1, "s", 0, 288)
-            stage1(1, 4)
-            mx(2, X, 4)
-            quant_c(1, Y)
-            mx(2, X, 2)
-            mx(3, Y, 3)
-            quant_c(0, Y)
-            mx(1, Y, 3)
-            leave(2, X, "s")
-            mx(3, Y, 1)
-            quant_act(2, 1)
+            mx(0, X, 0)
+            perm_w(2, 1)
+            mx(1, X, 4)
+            mx(1, X, 0)
+            prod_w(1, 4)
+            mx(1, X, 2)
+            inter(3, 1, "s", 288, 576)
+            tr_w(1, 0)
+            prod_w(1, 1)
+            mx(1, X, 3)
+            stage1(0, 6)
+            tr_w(2, 3)
+            leave(0, X, "s")
+            tr_w(2, 5)
+            quant_w(1, 2)
+            leave(1, X, "s")
+            tr_w(2, 4)
+            prod_w(1, 0)
             inter(3, 1, "s", 0, 288)
-            mx(3, Y, 0)
-            mx(0, Y, 0)
-            inter(3, 1, "v", 288, 576)
-            mx(1, Y, 0)
-            mx(0, Y, 3)
-            mx(1, Y, 4)
-            quant_act(0, 1)
-            mx(1, Y, 1)
-            cast_w(2, 1)
-            mx(0, Y, 1)
-            mx(3, Y, 4)
+            mx(2, X, 4)
+            mx(2, X, 5)
+            mx(3, X, 4)
+            quant_w(1, 1)
+            tr_w(2, 2)
+            inter(0, 1, "s", 0, 288)
+            quant_w(1, 0)
+            mx(3, X, 3)
+            mx(3, X, 5)
             quant_act(3, 1)
+            mx(2, X, 3)
+            mx(2, X, 0)
+            exit_c(0, 5)
+            mx(2, X, 2)
+            inter(1, 1, "s", 288, 576)
+            mx(3, X, 2)
+            mx(2, X, 1)
+            exit_c(0, 6)
+            mx(3, X, 0)
+            mx(3, X, 1)
+            quant_c(1, Y)
+            stage1(0, 4)
+            leave(2, X, "s")
+            mx(3, Y, 5)
+            quant_act(1, 1)
+            mx(3, Y, 1)
+            leave(3, X, "s")
+            mx(2, Y, 5)
+            quant_c(0, Y)
+            mx(2, Y, 1)
+            cast_w(2, 0)
+            mx(3, Y, 3)
+            quant_act(0, 1)
+            mx(1, Y, 5)
+            mx(2, Y, 0)
+            mx(3, Y, 0)
+            inter(2, 1, "s", 288, 576)
+            inter(2, 1, "v", 0, 288)
+            mx(2, Y, 3)
             mx(1, Y, 2)
+            mx(1, Y, 0)
+            exit_c(0, 4)
+            mx(1, Y, 1)
             mx(3, Y, 2)
             cast_w(3, 2)
-            exit_c(1, 4)
-            mx(0, Y, 2)
-            mx(3, Y, 5)
-            prod_w(2, 1)
-            mx(1, Y, 5)
-            mx(2, Y, 2)
-            leave(3, Y, "s")
-            mx(0, Y, 4)
-            mx(2, Y, 1)
-            leave(1, Y, "s")
-            quant_c(0, Z)
-            mx(2, Y, 4)
             quant_c(1, Z)
-            mx(2, Y, 0)
-            prod_w(2, 0)
-            perm_w(2, 1)
-            mx(0, Z, 0)
-            mx(1, Z, 0)
-            mx(1, Z, 2)
-            mx(0, Z, 2)
-            mx(1, Z, 4)
-            mx(0, Z, 3)
-            mx(2, Y, 5)
             mx(0, Y, 5)
+            quant_act(2, 1)
+            mx(0, Y, 3)
+            mx(0, Y, 0)
+            prod_w(2, 4)
+            mx(2, Y, 2)
+            perm_w(2, 0)
+            mx(3, Y, 4)
+            mx(2, Y, 4)
+            mx(0, Y, 4)
+            quant_c(0, Z)
+            mx(0, Y, 2)
             prod_w(2, 5)
-            perm_w(3, 2)
-            mx(0, Z, 5)
-            mx(0, Z, 1)
+            leave(3, Y, "s")
+            mx(1, Y, 4)
+            mx(1, Y, 3)
+            leave(2, Y, "s")
+            mx(3, Z, 0)
+            mx(3, Z, 2)
+            mx(3, Z, 5)
+            mx(3, Z, 4)
+            mx(0, Y, 1)
+            prod_w(2, 3)
+            leave(1, Y, "s")
+            mx(3, Z, 1)
+            mx(3, Z, 3)
+            mx(2, Z, 3)
+            mx(2, Z, 2)
+            mx(2, Z, 5)
+            mx(2, Z, 1)
+            leave(0, Y, "s")
+            mx(2, Z, 4)
             mx(1, Z, 5)
             mx(1, Z, 1)
-            mx(0, Z, 4)
-            mx(1, Z, 3)
-            mx(2, Y, 3)
-            tr_w(2, 2)
-            leave(0, Y, "s")
-            leave(0, Z, "v")
-            tr_w(2, 3)
-            quant_w(2, 0)
-            tr_w(3, 4)
-            leave(2, Y, "s")
-            prod_w(2, 4)
-            mx(3, Z, 3)
-            mx(3, Z, 4)
-            mx(3, Z, 2)
-            leave(1, Z, "s")
-            mx(3, Z, 1)
-            mx(3, Z, 0)
-            cast_w(3, 1)
-            mx(2, Z, 4)
-            mx(2, Z, 3)
-            store(1, 2)
-            mx(5, X, 1)
-            mx(2, Z, 2)
-            mx(3, Z, 5)
-            mx(2, Z, 1)
-            prod_w(2, 2)
-            mx(4, Y, 1)
-            mx(2, Z, 5)
-            mx(5, X, 0)
-            leave(3, Z, "s")
-            perm_w(3, 1)
-            mx(4, Y, 0)
-            store(3, 1)
             mx(2, Z, 0)
-            mx(5, Y, 1)
-            prod_w(2, 3)
-            mx(5, Y, 0)
-            tr_w(3, 5)
-            leave(2, Z, "s")
-            cast_w(3, 0)
-            tr_w(3, 3)
-            store(2, 2)
-            store(0, 0)
+            mx(1, Z, 0)
+            mx(1, Z, 4)
+            mx(1, Z, 3)
+            prod_w(2, 2)
+            perm_w(3, 2)
+            mx(1, Z, 2)
+            mx(0, Z, 3)
+            mx(0, Z, 2)
+            mx(0, Z, 4)
+            mx(0, Z, 5)
+            mx(0, Z, 1)
+            mx(0, Z, 0)
+            tr_w(2, 0)
+            tr_w(2, 1)
             quant_w(2, 2)
-            store(0, 2)
-            store(2, 0)
-            tr_w(3, 2)
-            store(3, 2)
-            store(3, 0)
-            store(1, 1)
-            mx(4, X, 0)
+            leave(1, Z, "s")
+            leave(2, Z, "s")
+            tr_w(3, 5)
+            leave(3, Z, "s")
+            cast_w(3, 1)
+            tr_w(3, 4)
             quant_w(2, 1)
-            mx(5, X, 4)
-            store(0, 1)
-            mx(5, Y, 4)
-            prod_w(3, 5)
-            mx(4, X, 5)
-            mx(5, X, 3)
-            mx(5, X, 2)
-            mx(5, X, 5)
-            prod_w(3, 2)
-            mx(4, Y, 5)
-            leave(5, X, "s")
-            mx(4, Y, 3)
-            mx(4, X, 2)
-            perm_w(3, 0)
-            mx(4, X, 1)
-            prod_w(3, 4)
-            mx(4, Y, 4)
-            mx(4, Y, 2)
-            mx(5, Y, 5)
-            mx(4, Z, 0)
-            mx(4, X, 3)
-            prod_w(3, 3)
-            mx(4, Z, 2)
-            mx(4, Z, 5)
-            mx(5, Y, 3)
-            leave(4, Y, "s")
-            mx(5, Y, 2)
-            mx(4, Z, 4)
-            mx(4, X, 4)
-            quant_w(3, 2)
-            leave(5, Y, "s")
-            tr_w(3, 1)
-            tr_w(3, 0)
-            quant_w(3, 1)
-            leave(4, X, "s")
-            mx(4, Z, 1)
-            mx(6, Z, 4, "tr")
-            mx(5, Z, 3)
-            prod_w(3, 1)
-            mx(5, Z, 4)
-            mx(4, Z, 3)
-            mx(5, Z, 1)
-            mx(7, Z, 2, "tr")
-            mx(6, X, 5)
-            leave(4, Z, "s")
+            store(3, 2)
+            store(3, 1)
+            store(0, 0)
             mx(5, Z, 5)
-            mx(5, Z, 0)
-            store(4, 2)
-            mx(7, Z, 3, "tr")
-            store(4, 0)
-            mx(6, X, 3)
-            store(5, 0)
+            mx(5, X, 4)
+            prod_w(2, 0)
+            mx(4, X, 4)
+            leave(0, Z, "s")
+            mx(5, X, 5)
+            perm_w(3, 1)
+            mx(5, Z, 3)
+            store(0, 2)
+            mx(4, X, 3)
+            store(1, 2)
+            store(2, 2)
+            store(1, 1)
+            mx(4, X, 5)
+            prod_w(2, 1)
             store(2, 1)
+            mx(5, Z, 4)
+            mx(5, X, 2)
+            cast_w(3, 0)
+            mx(5, Y, 2)
+            mx(5, Y, 5)
+            mx(5, X, 3)
+            store(1, 0)
+            quant_w(2, 0)
+            mx(4, X, 2)
+            tr_w(3, 3)
+            perm_w(3, 0)
+            prod_w(3, 5)
+            tr_w(3, 2)
+            mx(5, Z, 1)
+            mx(5, Y, 0)
+            mx(5, Z, 0)
+            mx(5, Z, 2)
+            mx(5, X, 0)
+            prod_w(3, 4)
+            leave(5, Z, "s")
+            mx(4, X, 1)
+            mx(5, X, 1)
+            mx(5, Y, 1)
+            leave(5, X, "s")
+            mx(4, Z, 2)
+            prod_w(3, 3)
+            mx(4, Z, 5)
+            mx(4, Z, 3)
+            mx(4, Z, 1)
+            mx(4, X, 0)
+            mx(5, Y, 4)
+            mx(4, Z, 4)
+            mx(4, Z, 0)
+            tr_w(3, 1)
+            prod_w(3, 2)
+            leave(4, Z, "s")
+            leave(4, X, "s")
+            tr_w(3, 0)
+            store(4, 1)
+            store(5, 1)
+            mx(4, Y, 5)
+            store(4, 0)
+            mx(5, Y, 3)
+            store(2, 0)
+            quant_w(3, 2)
+            store(5, 0)
+            store(0, 1)
+            mx(4, Y, 1)
+            leave(5, Y, "s")
+            mx(4, Y, 0)
+            quant_w(3, 1)
+            mx(4, Y, 2)
+            mx(4, Y, 4)
+            store(5, 2)
+            store(3, 0)
             prod_w(3, 0)
-            mx(6, X, 4)
-            mx(6, Y, 3)
-            mx(6, Z, 5, "tr")
-            mx(6, Z, 2, "tr")
+            mx(4, Y, 3)
+            mx(6, Z, 4, "tr")
             mx(7, Y, 4)
-            mx(6, Z, 3, "tr")
-            mx(7, Z, 4, "tr")
+            leave(4, Y, "s")
+            mx(6, X, 4)
+            mx(6, Z, 2, "tr")
+            mx(7, Y, 3)
+            prod_w(3, 1)
+            store(4, 2)
+            mx(6, Z, 5, "tr")
+            mx(6, Y, 3)
+            mx(6, X, 3)
+            mx(7, Y, 2)
+            mx(7, X, 4)
             mx(6, Y, 5)
             quant_w(3, 0)
-            mx(6, Y, 2)
+            mx(7, X, 2)
+            mx(6, Z, 3, "tr")
+            mx(6, X, 5)
             mx(6, X, 2)
-            mx(5, Z, 2)
-            mx(7, Y, 3)
-            leave(5, Z, "v")
-            mx(6, Z, 1, "tr")
-            mx(7, Z, 5, "tr")
+            mx(7, X, 5)
+            mx(6, Y, 4)
+            mx(7, X, 1)
+            mx(7, X, 0)
+            mx(7, X, 3)
+            mx(6, Y, 1)
+            leave(7, X, "v")
             mx(6, X, 0)
             mx(6, X, 1)
-            mx(7, Y, 2)
-            mx(7, Z, 0, "tr")
-            mx(7, Z, 1, "tr")
-            mx(6, Y, 0)
-            leave(7, Z, "v")
-            mx(6, Z, 0, "tr")
-            mx(7, X, 3)
-            leave(6, X, "v")
-            leave(6, Z, "s")
-            mx(7, X, 1)
-            mx(6, Y, 4)
-            mx(6, Y, 1)
-            store(6, 0)
-            store(5, 1)
-            store(7, 1)
-            mx(7, Y, 1)
-            store(5, 2)
-            leave(6, Y, "v")
-            mx(7, Y, 5)
-            mx(7, Y, 0)
-            mx(7, X, 4)
-            store(6, 2)
-            leave(7, Y, "v")
-            store(4, 1)
-            mx(7, X, 2)
-            store(6, 1)
-            mx(7, X, 5)
-            mx(7, X, 0)
-            store(7, 2)
-            leave(7, X, "s")
+            mx(6, Z, 1, "tr")
+            mx(6, Y, 2)
             store(7, 0)
+            leave(6, X, "s")
+            mx(6, Y, 0)
+            mx(6, Z, 0, "tr")
+            mx(7, Y, 1)
+            leave(6, Y, "v")
+            store(6, 0)
+            leave(6, Z, "s")
+            mx(7, Y, 0)
+            store(6, 1)
+            mx(7, Y, 5)
+            mx(7, Z, 3, "tr")
+            mx(7, Z, 5, "tr")
+            store(6, 2)
+            mx(7, Z, 2, "tr")
+            mx(7, Z, 0, "tr")
+            leave(7, Y, "s")
+            mx(7, Z, 4, "tr")
+            mx(7, Z, 1, "tr")
+            leave(7, Z, "v")
+            store(7, 2)
+            store(7, 1)

from contextlib import ExitStack

import concourse.mybir as mybir
from concourse.masks import make_identity

F32 = mybir.dt.float32
BF16 = mybir.dt.bfloat16
U32 = mybir.dt.uint32
U8 = mybir.dt.uint8
FP8 = mybir.dt.float8_e4m3fn
FP8X4 = mybir.dt.float8_e4m3fn_x4
MULT = mybir.AluOpType.mult
ADD = mybir.AluOpType.add
SUB = mybir.AluOpType.subtract
POW = mybir.AluOpType.pow
IDENT = mybir.ActivationFunctionType.Identity

P = 128
B, CV, CH, CO, HW = 2, 512, 2048, 1024, 576
CF = CO + CH
N = B * HW
MT = CO // P
NQ = MT // 2
GC = CO // 512
GH = CH // 512
G = GC + GH
EPS = 1e-5
FLOPS = 2 * CO * CV * N + 2 * CO * CF * N

X, Z, Y = (0, 512), (512, 128), (640, 512)
CTX = -1


def tile_afnb_pb_kernel(tc, context, high, ww, bw, wf_bytes, wf_scale, bfuse, gf, bef, mf, vf, out):
    nc = tc.nc
    with ExitStack() as ctx:
        keep = ctx.enter_context(tc.tile_pool(name="keep", bufs=1))
        rot = ctx.enter_context(tc.tile_pool(name="rot", bufs=3))
        psum = ctx.enter_context(tc.psum_pool(name="psum", bufs=4))

        wf_t = wf_bytes.rearrange("(q m p) k -> q p m k", p=P, m=2)
        ww_t = ww.rearrange("(g p t) k -> g p t k", g=GC, t=4)
        ctx_t = context.rearrange("b (p t) h w -> b p t (h w)", t=4)
        high_t = high.rearrange("b (g p t) h w -> b g p t (h w)", p=P, t=4)
        wbytes, raws = {}, {}
        wwr = {}

        def load_w(q, m, lo=0, hi=CF):
            if q not in wbytes:
                wbytes[q] = rot.tile([P, 2, CF], U8, name="wbytes", bufs=3)
            nc.sync.dma_start(out=wbytes[q][:, m, lo:hi], in_=wf_t[q, :, m, lo:hi])

        def load_ww(g):
            wwr[g] = rot.tile([P, 4, CV], BF16, name="wb", bufs=6)
            nc.sync.dma_start(out=wwr[g][:], in_=ww_t[g])

        def load_act(g, b, lo=0, hi=HW):
            if (g, b) not in raws:
                raws[g, b] = rot.tile([P, 4, HW], BF16, name="raw", bufs=8)
            src = ctx_t[b] if g == CTX else high_t[b, g]
            nc.sync.dma_start(out=raws[g, b][:, :, lo:hi], in_=src[:, :, lo:hi])

        ident = keep.tile([P, P], F32, name="ident")
        rows = keep.tile([P, P], BF16, name="rows")
        rows32 = keep.tile([P, P], F32, name="rows32")
        ws = keep.tile([P, G, 4], F32, name="ws")
        bwt = keep.tile([P, GC, 4], BF16, name="bwt")
        bn = keep.tile([P, 5 * MT], F32, name="bn")
        bn_scale = keep.tile([P, MT], F32, name="bn_scale")
        bn_bias = keep.tile([P, MT], F32, name="bn_bias")
        half = keep.tile([P, MT], F32, name="half")
        rstd = keep.tile([P, MT], F32, name="rstd")
        bdiff = keep.tile([P, MT], F32, name="bdiff")

        warm_in = keep.tile([P, 512], BF16, name="warm_in")

        def load_consts():
            nc.vector.memset(warm_in[:], 0.0)
            make_identity(nc, ident[:])
            nc.gpsimd.memset(rows[:], 0.0)
            for i, v in enumerate((bfuse, gf, bef, mf, vf)):
                nc.gpsimd.dma_start(out=rows[MT * i : MT * (i + 1), :], in_=v.rearrange("(m p) -> m p", p=P))
            nc.scalar.dma_start(out=ws[:], in_=wf_scale.rearrange("o (g p t) -> p (o g) t", p=P, t=4))
            nc.scalar.dma_start(out=bwt[:], in_=bw.rearrange("(g p t) -> p g t", p=P, t=4))

        def make_consts():
            nc.gpsimd.tensor_copy(out=rows32[:], in_=rows[:])
            nc.gpsimd.memset(half[:], -0.5)

        const_bank = []

        def tr_consts():
            bank = psum.tile([P, 2, 2 * P], F32, name="tr")
            const_bank.append(bank)
            nc.tensor.transpose(bank[:, 0, 0:P], rows32[:], ident[:])

        def exit_consts():
            nc.scalar.copy(out=bn[:], in_=const_bank[0][:, 0, 0 : 5 * MT])

        def consts():
            col = [bn[:, MT * i : MT * (i + 1)] for i in range(5)]
            nc.gpsimd.tensor_scalar(out=rstd[:], in0=col[4], scalar1=EPS, scalar2=None, op0=ADD)
            nc.gpsimd.tensor_tensor(out=rstd[:], in0=rstd[:], in1=half[:], op=POW)
            nc.gpsimd.tensor_tensor(out=bn_scale[:], in0=col[1], in1=rstd[:], op=MULT)
            nc.gpsimd.tensor_tensor(out=bdiff[:], in0=col[0], in1=col[3], op=SUB)
            nc.gpsimd.tensor_tensor(out=bdiff[:], in0=bdiff[:], in1=bn_scale[:], op=MULT)
            nc.gpsimd.tensor_tensor(out=bn_bias[:], in0=bdiff[:], in1=col[2], op=ADD)

        def quant(codes, scales, src, lo, n):
            nc.vector.quantize_mx(out=codes[:, lo : lo + n].bitcast(FP8X4), scales=scales[:, lo : lo + n], in_=src)

        act_c = [keep.tile([P, N], U32, name="act_c%d" % g, align_bytes=64) for g in range(G)]
        act_s = [keep.tile([P, N], U8, name="act_s%d" % g, align_bytes=64) for g in range(G)]
        ctx_c = keep.tile([P, N], U32, name="ctx_c", align_bytes=64)
        ctx_s = keep.tile([P, N], U8, name="ctx_s", align_bytes=64)
        grps = {}

        def inter(g, b, eng="s", lo=0, hi=HW):
            if (g, b) not in grps:
                grps[g, b] = rot.tile([P, HW, 4], BF16, name="grp", bufs=4, align_bytes=64)
            dst = grps[g, b][:, lo:hi, :].rearrange("p (c i) t -> p c t i", i=4)
            src = raws[g, b][:, :, lo:hi].rearrange("p t (c i) -> p c t i", i=4)
            if eng == "v":
                nc.vector.tensor_copy(out=dst, in_=src)
            elif eng == "g":
                nc.gpsimd.tensor_scalar(out=dst, in0=src, scalar1=1.0, scalar2=0.0, op0=MULT, op1=ADD)
            else:
                nc.scalar.copy(out=dst, in_=src)

        def quant_act(g, b):
            c, s = (ctx_c, ctx_s) if g == CTX else (act_c[GC + g], act_s[GC + g])
            flat = grps[g, b][:].rearrange("p n t -> p (n t)")
            quant(c, s, flat[:, 0:2048], b * HW, 512)
            quant(c, s, flat[:, 2048:2304], b * HW + 512, 64)

        wwg = {}
        wwc = keep.tile([P, CO], U32, name="wwc", align_bytes=64)
        wwsc = keep.tile([P, CO], U8, name="wwsc", align_bytes=64)
        ww_bank = {}

        def heat(bank, times):
            for i in range(times):
                nc.tensor.matmul(bank, lhsT=warm_in[:, 0:P], rhs=warm_in[:], start=True, stop=True)

        def warm(i):
            bank = psum.tile([P, 2, 2 * P], F32, name="tr")
            heat(bank[:].rearrange("p u r -> p (u r)"), 1)

        def tr_ww(i, warm=0):
            ww_bank[i] = psum.tile([P, 2, 2, P], F32, name="tr")
            heat(ww_bank[i][:].rearrange("p c u r -> p (c u r)"), warm)
            for j in range(2):
                g, t = divmod(2 * i + j, 4)
                words = wwr[g][:, t, :].bitcast(F32)
                for u in range(2):
                    nc.tensor.transpose(ww_bank[i][:, j, u, :], words[:, u : CV // 2 : 2], ident[:])

        def exit_ww(i, eng):
            g, t = divmod(2 * i, 4)
            if g not in wwg:
                wwg[g] = rot.tile([P, 4, 512], BF16, name="wg", bufs=5, align_bytes=64)
            dst = wwg[g][:, t : t + 2, :].bitcast(F32).rearrange("p c (r u) -> p c r u", u=2)
            src = ww_bank[i][:].rearrange("p c u r -> p c r u")
            if eng == "v":
                nc.vector.tensor_copy(out=dst, in_=src)
            else:
                nc.scalar.copy(out=dst, in_=src)

        def quant_ww(g):
            quant(wwc, wwsc, wwg[g][:].rearrange("p c k -> p (c k)"), 512 * g, 512)

        cgrp, cbank = {}, {}

        def stage1(g, nb):
            bank = psum.tile([P, 4, P], F32, name="acc")
            cbank[g, nb] = bank
            n = slice(nb * P, (nb + 1) * P)
            for t in range(4):
                k = slice((4 * g + t) * P, (4 * g + t + 1) * P)
                nc.tensor.matmul_mx(
                    out=bank[:, t, :], lhsT=wwc[:, k].bitcast(FP8X4), lhsT_scale=wwsc[:, k],
                    rhs=ctx_c[:, n].bitcast(FP8X4), rhs_scale=ctx_s[:, n], start=True, stop=True)

        def exit_c(g, nb):
            lo, n = X if nb < 4 else Z if nb < 5 else Y
            if (g, lo) not in cgrp:
                cgrp[g, lo] = rot.tile([P, n, 4], BF16, name="cgrp", bufs=4, align_bytes=64)
            off = nb * P - lo
            nc.vector.tensor_tensor(
                out=cgrp[g, lo][:, off : off + P, :], in0=cbank[g, nb][:].rearrange("p t n -> p n t"),
                in1=bwt[:, g, :].unsqueeze(1).to_broadcast([P, P, 4]), op=ADD)

        def quant_c(g, chunk):
            lo, n = chunk
            quant(act_c[g], act_s[g], cgrp[g, lo][:].rearrange("p n t -> p (n t)"), lo, n)

        wb, wg, wbank = {}, {}, {}
        wc = [keep.tile([P, G, 2 * P], U32, name="wc%d" % q, align_bytes=64) for q in range(NQ)]
        wsc = [keep.tile([P, G, 2 * P], U8, name="wsc%d" % q, align_bytes=64) for q in range(NQ)]

        def cast_w(q, h):
            wb[q, h] = rot.tile([P, 2, 1024], BF16, name="wb", bufs=6)
            for m in range(2):
                nc.scalar.copy(out=wb[q, h][:, m], in_=wbytes[q][:, m, 1024 * h : 1024 * (h + 1)].bitcast(FP8))

        wp = {}

        def perm_w(q, h):
            wp[q, h] = rot.tile([P, 2, 1024], BF16, name="wb", bufs=6)
            nc.scalar.copy(
                out=wp[q, h][:].rearrange("p m k -> p (m k)").bitcast(F32).rearrange("p (g u w) -> p g u w", u=2, w=P),
                in_=wb[q, h][:].rearrange("p m k -> p (m k)").bitcast(F32).rearrange("p (g w u) -> p g u w", u=2, w=P))

        def tr_w(q, g, warm=0):
            h, j = divmod(g, 2)
            bank = psum.tile([P, 2, 2 * P], F32, name="tr")
            wbank[q, g] = bank
            heat(bank[:].rearrange("p u r -> p (u r)"), warm)
            for m in range(2):
                words = (wp if (q, h) in wp else wb)[q, h][:, m].bitcast(F32)
                for u in range(2):
                    cols = slice(256 * j + P * u, 256 * j + P * (u + 1)) if (q, h) in wp else slice(256 * j + u, 256 * (j + 1), 2)
                    nc.tensor.transpose(bank[:, u, m * P : (m + 1) * P], words[:, cols], ident[:])

        def prod_w(q, g):
            h, j = divmod(g, 2)
            if (q, h) not in wg:
                wg[q, h] = rot.tile([P, 2, 1024], BF16, name="wg", bufs=5, align_bytes=64)
            nc.vector.tensor_tensor(
                out=wg[q, h][:, j].rearrange("p (r u e) -> p r u e", u=2, e=2),
                in0=wbank[q, g][:].bitcast(BF16).rearrange("p u (r e) -> p r u e", e=2),
                in1=ws[:, g, :].rearrange("p (u e) -> p u e", e=2).unsqueeze(1).to_broadcast([P, 2 * P, 2, 2]),
                op=MULT)

        def quant_w(q, h):
            flat = wg[q, h][:].rearrange("p j k -> p (j k)")
            quant(wc[q][:].rearrange("p g r -> p (g r)"), wsc[q][:].rearrange("p g r -> p (g r)"), flat, 512 * h, 512)

        out_v = out.rearrange("b (m p) h w -> m b p (h w)", p=P)
        accs, outs = {}, {}

        def mx(m, chunk, g, tag="acc"):
            lo, n = chunk
            if (m, lo) not in accs:
                accs[m, lo] = [psum.tile([P, n], F32, name=tag), 0]
            acc, done = accs[m, lo]
            q, r = divmod(m, 2)
            k = slice(r * P, (r + 1) * P)
            nc.tensor.matmul_mx(
                out=acc[:], lhsT=wc[q][:, g, k].bitcast(FP8X4), lhsT_scale=wsc[q][:, g, k],
                rhs=act_c[g][:, lo : lo + n].bitcast(FP8X4), rhs_scale=act_s[g][:, lo : lo + n],
                start=(done == 0), stop=(done == G - 1))
            accs[m, lo][1] = done + 1

        def leave(m, chunk, eng="s"):
            lo, n = chunk
            part = 0 if lo == 0 else 1
            if (m, part) not in outs:
                outs[m, part] = rot.tile([P, (512, 640)[part]], F32, name="out%d" % part, bufs=4)
            dst = outs[m, part][:, lo - 512 * part : lo - 512 * part + n]
            acc = accs[m, lo][0]
            if eng == "v":
                nc.vector.tensor_scalar(out=dst, in0=acc[:], scalar1=bn_scale[:, m : m + 1], scalar2=bn_bias[:, m : m + 1], op0=MULT, op1=ADD)
            else:
                nc.scalar.activation(out=dst, in_=acc[:], func=IDENT, bias=bn_bias[:, m : m + 1], scale=bn_scale[:, m : m + 1])

        def store(m, part):
            if part == 0:
                nc.sync.dma_start(out=out_v[m, 0, :, 0:512], in_=outs[m, 0][:])
            elif part == 1:
                nc.sync.dma_start(out=out_v[m, 0, :, 512:576], in_=outs[m, 1][:, 0:64])
            else:
                nc.sync.dma_start(out=out_v[m, 1], in_=outs[m, 1][:, 64:640])

        load_consts()
        load_w(0, 0, 0, 1024)
        load_w(0, 1, 0, 1024)
        load_w(0, 0, 2048, 3072)
        load_w(0, 1, 2048, 3072)
        load_act(CTX, 0, 288, 576)
        load_act(CTX, 1)
        load_w(0, 1, 1024, 2048)
        load_act(CTX, 0, 0, 288)
        load_w(0, 0, 1024, 2048)
        load_ww(1)
        load_act(3, 0)
        load_w(1, 0)
        load_w(1, 1)
        load_ww(0)
        load_act(0, 0)
        load_act(2, 0)
        load_w(2, 1)
        load_act(3, 1)
        load_act(0, 1)
        load_w(2, 0)
        load_act(1, 0)
        load_act(1, 1)
        load_w(3, 0)
        load_act(2, 1)
        load_w(3, 1)
        with tc.manual_schedule(engines={mybir.EngineType.PE, mybir.EngineType.DVE, mybir.EngineType.Activation}):
            warm(1)
            warm(4)
            warm(12)
            warm(15)
            warm(6)
            warm(8)
            cast_w(0, 0)
            warm(19)
            cast_w(0, 2)
            inter(CTX, 0, "v", 288, 576)
            tr_w(0, 0)
            tr_w(0, 1)
            prod_w(0, 0)
            warm(23)
            inter(CTX, 1, "s", 0, 288)
            warm(2)
            prod_w(0, 1)
            make_consts()
            tr_w(0, 4)
            inter(CTX, 0, "s", 0, 288)
            inter(CTX, 1, "v", 288, 576)
            tr_ww(3)
            prod_w(0, 4)
            tr_ww(2)
            cast_w(0, 1)
            tr_w(0, 5)
            quant_act(CTX, 0)
            exit_ww(3, "s")
            tr_w(0, 3)
            quant_w(0, 0)
            exit_ww(2, "s")
            quant_act(CTX, 1)
            inter(3, 0, "s", 0, 288)
            tr_w(0, 2)
            quant_ww(1)
            prod_w(0, 5)
            cast_w(1, 1)
            stage1(1, 3)
            stage1(1, 0)
            prod_w(0, 3)
            cast_w(1, 2)
            tr_ww(0)
            tr_w(1, 3)
            prod_w(0, 2)
            cast_w(1, 0)
            stage1(1, 6)
            stage1(1, 2)
            quant_w(0, 2)
            exit_ww(0, "s")
            exit_c(1, 3)
            inter(0, 0, "s", 0, 288)
            exit_c(1, 6)
            stage1(1, 4)
            tr_ww(1)
            exit_c(1, 0)
            inter(3, 0, "s", 288, 576)
            warm(16)
            prod_w(1, 3)
            stage1(1, 1)
            quant_w(0, 1)
            exit_ww(1, "s")
            tr_consts()
            stage1(1, 8)
            exit_c(1, 2)
            inter(0, 0, "s", 288, 576)
            quant_ww(0)
            stage1(1, 5)
            warm(21)
            exit_c(1, 4)
            exit_consts()
            inter(2, 0, "s", 288, 576)
            consts()
            exit_c(1, 1)
            stage1(0, 3)
            tr_w(1, 5)
            exit_c(1, 5)
            inter(2, 0, "s", 0, 288)
            exit_c(1, 8)
            stage1(0, 2)
            exit_c(0, 3)
            stage1(0, 8)
            stage1(0, 1)
            quant_c(1, X)
            stage1(0, 7)
            inter(1, 0, "s", 288, 576)
            tr_w(1, 4)
            exit_c(0, 1)
            tr_w(1, 2)
            exit_c(0, 2)
            cast_w(2, 2)
            quant_act(3, 0)
            stage1(1, 7)
            exit_c(0, 8)
            inter(1, 0, "s", 0, 288)
            exit_c(0, 7)
            stage1(0, 0)
            prod_w(1, 5)
            mx(0, X, 5)
            cast_w(2, 1)
            tr_w(1, 1)
            quant_act(0, 0)
            inter(0, 1, "s", 288, 576)
            quant_act(2, 0)
            mx(1, X, 1)
            mx(0, X, 1)
            mx(0, X, 2)
            exit_c(0, 0)
            mx(0, X, 4)
            perm_w(2, 2)
            quant_act(1, 0)
            quant_c(0, X)
            mx(0, X, 3)
            inter(1, 1, "s", 0, 288)
            mx(1, X, 5)
            exit_c(1, 7)
            prod_w(1, 2)
            stage1(0, 5)
            mx(0, X, 0)
            perm_w(2, 1)
            mx(1, X, 4)
            mx(1, X, 0)
            prod_w(1, 4)
            mx(1, X, 2)
            inter(3, 1, "s", 288, 576)
            tr_w(1, 0)
            prod_w(1, 1)
            mx(1, X, 3)
            stage1(0, 6)
            tr_w(2, 3)
            leave(0, X, "s")
            tr_w(2, 5)
            quant_w(1, 2)
            leave(1, X, "s")
            tr_w(2, 4)
            prod_w(1, 0)
            inter(3, 1, "s", 0, 288)
            mx(2, X, 4)
            mx(2, X, 5)
            mx(3, X, 4)
            quant_w(1, 1)
            tr_w(2, 2)
            inter(0, 1, "s", 0, 288)
            quant_w(1, 0)
            mx(3, X, 3)
            mx(3, X, 5)
            quant_act(3, 1)
            mx(2, X, 3)
            mx(2, X, 0)
            exit_c(0, 5)
            mx(2, X, 2)
            inter(1, 1, "s", 288, 576)
            mx(3, X, 2)
            mx(2, X, 1)
            exit_c(0, 6)
            mx(3, X, 0)
            mx(3, X, 1)
            quant_c(1, Y)
            stage1(0, 4)
            leave(2, X, "s")
            mx(3, Y, 5)
            quant_act(1, 1)
            mx(3, Y, 1)
            leave(3, X, "s")
            mx(2, Y, 5)
            quant_c(0, Y)
            mx(2, Y, 1)
            cast_w(2, 0)
            mx(3, Y, 3)
            quant_act(0, 1)
            mx(1, Y, 5)
            mx(2, Y, 0)
            mx(3, Y, 0)
            inter(2, 1, "s", 288, 576)
            inter(2, 1, "v", 0, 288)
            mx(2, Y, 3)
            mx(1, Y, 2)
            mx(1, Y, 0)
            exit_c(0, 4)
            mx(1, Y, 1)
            mx(3, Y, 2)
            cast_w(3, 2)
            quant_c(1, Z)
            mx(0, Y, 5)
            quant_act(2, 1)
            mx(0, Y, 3)
            mx(0, Y, 0)
            prod_w(2, 4)
            mx(2, Y, 2)
            perm_w(2, 0)
            mx(3, Y, 4)
            mx(2, Y, 4)
            mx(0, Y, 4)
            quant_c(0, Z)
            mx(0, Y, 2)
            prod_w(2, 5)
            leave(3, Y, "s")
            mx(1, Y, 4)
            mx(1, Y, 3)
            leave(2, Y, "s")
            mx(3, Z, 0)
            mx(3, Z, 2)
            mx(3, Z, 5)
            mx(3, Z, 4)
            mx(0, Y, 1)
            prod_w(2, 3)
            leave(1, Y, "s")
            mx(3, Z, 1)
            mx(3, Z, 3)
            mx(2, Z, 3)
            mx(2, Z, 2)
            mx(2, Z, 5)
            mx(2, Z, 1)
            leave(0, Y, "s")
            mx(2, Z, 4)
            mx(1, Z, 5)
            mx(1, Z, 1)
            mx(2, Z, 0)
            mx(1, Z, 0)
            mx(1, Z, 4)
            mx(1, Z, 3)
            prod_w(2, 2)
            perm_w(3, 2)
            mx(1, Z, 2)
            mx(0, Z, 3)
            mx(0, Z, 2)
            mx(0, Z, 4)
            mx(0, Z, 5)
            mx(0, Z, 1)
            mx(0, Z, 0)
            tr_w(2, 0)
            tr_w(2, 1)
            quant_w(2, 2)
            leave(1, Z, "s")
            leave(2, Z, "s")
            tr_w(3, 5)
            leave(3, Z, "s")
            cast_w(3, 1)
            tr_w(3, 4)
            quant_w(2, 1)
            store(3, 2)
            store(3, 1)
            store(0, 0)
            mx(5, Z, 5)
            mx(5, X, 4)
            prod_w(2, 0)
            mx(4, X, 4)
            leave(0, Z, "s")
            mx(5, X, 5)
            perm_w(3, 1)
            mx(5, Z, 3)
            store(0, 2)
            mx(4, X, 3)
            store(1, 2)
            store(2, 2)
            store(1, 1)
            mx(4, X, 5)
            prod_w(2, 1)
            store(2, 1)
            mx(5, Z, 4)
            mx(5, X, 2)
            cast_w(3, 0)
            mx(5, Y, 2)
            mx(5, Y, 5)
            mx(5, X, 3)
            store(1, 0)
            quant_w(2, 0)
            mx(4, X, 2)
            tr_w(3, 3)
            perm_w(3, 0)
            prod_w(3, 5)
            tr_w(3, 2)
            mx(5, Z, 1)
            mx(5, Y, 0)
            mx(5, Z, 0)
            mx(5, Z, 2)
            mx(5, X, 0)
            prod_w(3, 4)
            leave(5, Z, "s")
            mx(4, X, 1)
            mx(5, X, 1)
            mx(5, Y, 1)
            leave(5, X, "s")
            mx(4, Z, 2)
            prod_w(3, 3)
            mx(4, Z, 5)
            mx(4, Z, 3)
            mx(4, Z, 1)
            mx(4, X, 0)
            mx(5, Y, 4)
            mx(4, Z, 4)
            mx(4, Z, 0)
            tr_w(3, 1)
            prod_w(3, 2)
            leave(4, Z, "s")
            leave(4, X, "s")
            tr_w(3, 0)
            store(4, 1)
            store(5, 1)
            mx(4, Y, 5)
            store(4, 0)
            mx(5, Y, 3)
            store(2, 0)
            quant_w(3, 2)
            store(5, 0)
            store(0, 1)
            mx(4, Y, 1)
            leave(5, Y, "s")
            mx(4, Y, 0)
            quant_w(3, 1)
            mx(4, Y, 2)
            mx(4, Y, 4)
            store(5, 2)
            store(3, 0)
            prod_w(3, 0)
            mx(4, Y, 3)
            mx(6, Z, 4, "tr")
            mx(7, Y, 4)
            leave(4, Y, "s")
            mx(6, X, 4)
            mx(6, Z, 2, "tr")
            mx(7, Y, 3)
            prod_w(3, 1)
            store(4, 2)
            mx(6, Z, 5, "tr")
            mx(6, Y, 3)
            mx(6, X, 3)
            mx(7, Y, 2)
            mx(7, X, 4)
            mx(6, Y, 5)
            quant_w(3, 0)
            mx(7, X, 2)
            mx(6, Z, 3, "tr")
            mx(6, X, 5)
            mx(6, X, 2)
            mx(7, X, 5)
            mx(6, Y, 4)
            mx(7, X, 1)
            mx(7, X, 0)
            mx(7, X, 3)
            mx(6, Y, 1)
            leave(7, X, "v")
            mx(6, X, 0)
            mx(6, X, 1)
            mx(6, Z, 1, "tr")
            mx(6, Y, 2)
            store(7, 0)
            leave(6, X, "s")
            mx(6, Y, 0)
            mx(6, Z, 0, "tr")
            mx(7, Y, 1)
            leave(6, Y, "v")
            store(6, 0)
            leave(6, Z, "s")
            mx(7, Y, 0)
            store(6, 1)
            mx(7, Y, 5)
            mx(7, Z, 3, "tr")
            mx(7, Z, 5, "tr")
            store(6, 2)
            mx(7, Z, 2, "tr")
            mx(7, Z, 0, "tr")
            leave(7, Y, "s")
            mx(7, Z, 4, "tr")
            mx(7, Z, 1, "tr")
            leave(7, Z, "v")
            store(7, 2)
            store(7, 1)
